import numpy as np
import ml_dtypes


def mxq(x, axis, fmt="e4m3"):
    dtype, down = {"e4m3": (ml_dtypes.float8_e4m3fn, 7), "e5m2": (ml_dtypes.float8_e5m2, 14)}[fmt]
    v = np.moveaxis(np.asarray(x, np.float32).astype(ml_dtypes.bfloat16).astype(np.float64), axis, -1)
    blocks = v.reshape(v.shape[:-1] + (-1, 32))
    amax = np.abs(blocks).max(-1, keepdims=True)
    byte = np.maximum(np.where(amax > 0, np.frexp(amax)[1] - 1 + 127, 0) - down, 1)
    scale = np.exp2(byte - 127.0)
    codes = (blocks / scale).astype(np.float32).astype(dtype).astype(np.float64)
    return np.moveaxis((codes * scale).reshape(v.shape), -1, axis)


WIDE = False


def mx_kscale(k):
    if not WIDE:
        return np.ones(k)
    levels = np.array([10, -10, 5, -5, 0])
    a = np.random.permutation(np.resize(levels, k // 512 * 4)).reshape(k // 512, 4)
    idx = np.arange(k)
    return np.exp2(a[idx // 512, idx % 128 // 32])


BF16 = ml_dtypes.bfloat16


def bf(x):
    return np.asarray(x, np.float32).astype(BF16)


def f64(x):
    return np.asarray(x).astype(np.float64)


M, K, N, R = 4096, 512, 256, 16


def mix(rows, u, a, b):
    return a * (np.random.standard_normal((rows, R)) @ u) / np.sqrt(R) + b * np.random.standard_normal((rows, K))


def setup_inputs():
    s = mx_kscale(K)
    u = np.random.standard_normal((R, K))
    return {"x": bf(mix(M, u, 1.0, 0.5) * s),
            "weights": bf(mix(N, u, 1.0, 0.5) * (np.sqrt(R) / K) / s),
            "bias": bf(np.random.standard_normal(N) * 0.3),
            "center": bf(mix(N, u, 0.5, 0.1) * s),
            "sigma": bf(np.sqrt(np.sum(s * s)) * (1.0 + 0.1 * np.random.standard_normal(N)))}


def reference(x, weights, bias, center, sigma):
    x, weights, bias, center, sigma = f64(x), f64(weights), f64(bias), f64(center), f64(sigma)
    xq = mxq(x, 1, "e4m3")
    pw = (xq @ mxq(weights, 1, "e4m3").T) + bias
    wnorm = np.sqrt(np.sum(weights * weights, axis=1, keepdims=True))
    wn = weights / np.maximum(wnorm, 1e-12)
    pwc = (xq @ mxq(wn, 1, "e4m3").T) - np.sum(center * wn, axis=1)
    xn = (np.sum(x * x, axis=1, keepdims=True)
          + np.sum(center * center, axis=1)
          - 2.0 * (xq @ mxq(center, 1, "e4m3").T))
    poL2 = xn - pwc * pwc
    om = np.exp(-poL2 / (sigma * sigma))
    return pw * om

@@ -1,0 +1,304 @@
+from contextlib import ExitStack
+import math
+
+import concourse.masks as masks
+import concourse.mybir as mybir
+
+FP8X4 = mybir.dt.float8_e4m3fn_x4
+BF16 = mybir.dt.bfloat16
+F32 = mybir.dt.float32
+U32 = mybir.dt.uint32
+U8 = mybir.dt.uint8
+ALU = mybir.AluOpType
+ACT = mybir.ActivationFunctionType
+
+P = 128
+M, K, N = 4096, 512, 256
+FLOPS = 3 * 2 * M * K * N
+TPC = 4
+NCH = M // (P * TPC)
+CW = P * TPC
+R = math.sqrt(0.5)
+PINNED = True
+LAST_MUL_ON_VECTOR = True
+
+
+def tile_orthogonallyattenuatedlinear_t_kernel(tc, x, weights, bias, center, sigma, out):
+    nc = tc.nc
+    with ExitStack() as ctx:
+        const = ctx.enter_context(tc.tile_pool(name="const", bufs=1))
+        xpool = ctx.enter_context(tc.tile_pool(name="xpool", bufs=1))
+        work = ctx.enter_context(tc.tile_pool(name="work", bufs=2))
+        ps_x = ctx.enter_context(tc.psum_pool(name="ps_x", bufs=2))
+        ps_bc = ctx.enter_context(tc.psum_pool(name="ps_bc", bufs=3))
+        ps_a = ctx.enter_context(tc.psum_pool(name="ps_a", bufs=1))
+        ps_t = ctx.enter_context(tc.psum_pool(name="ps_t", bufs=2))
+        if PINNED:
+            ctx.enter_context(tc.manual_schedule())
+
+        xv = x.rearrange("(p c t) k -> p c (t k)", c=NCH, t=TPC)
+        ov = out.rearrange("(p c t) n -> p c (t n)", c=NCH, t=TPC)
+
+        w_sb = const.tile([P, 2 * K], BF16, name="w_sb")
+        c_sb = const.tile([P, 2 * K], BF16, name="c_sb")
+        vec = const.tile([P, 2 * N], BF16, name="vec")
+        nc.gpsimd.memset(vec[:], 0.0)
+        nc.scalar.dma_start(out=w_sb[:].rearrange("p (h k) -> p h k", h=2),
+                            in_=weights.rearrange("(h p) k -> p h k", h=2))
+        nc.scalar.dma_start(out=c_sb[:].rearrange("p (h k) -> p h k", h=2),
+                            in_=center.rearrange("(h p) k -> p h k", h=2))
+        nc.scalar.dma_start(out=vec[0:1, 0:N], in_=bias.unsqueeze(0))
+        nc.scalar.dma_start(out=vec[0:1, N:2 * N], in_=sigma.unsqueeze(0))
+        x_sb = []
+        for c in range(NCH):
+            xt_c = xpool.tile([P, TPC * K], BF16, name="x%d" % c)
+            nc.sync.dma_start(out=xt_c[:], in_=xv[:, c, :])
+            x_sb.append(xt_c)
+
+        one1 = const.tile([P, 1], F32, name="one1")
+        nc.vector.memset(one1[:], 1.0)
+        dummy = const.tile([P, 1], F32, name="dummy")
+        nc.scalar.activation(out=dummy[:], in_=one1[:], func=ACT.Sqrt)
+        ident_f = const.tile([P, P], F32, name="ident_f")
+        masks.make_identity(nc, ident_f[:])
+        ident_b = const.tile([P, P], BF16, name="ident_b")
+        masks.make_identity(nc, ident_b[:])
+        ones_b = const.tile([P, P], BF16, name="ones_b")
+        nc.vector.memset(ones_b[:], 1.0)
+        x2h = const.tile([P, NCH * TPC], F32, name="x2h")
+
+        def quantised(name, width):
+            codes = const.tile([P, width], U32, name=name + "_codes", align_bytes=64)
+            scales = const.tile([P, width], U8, name=name + "_scales", align_bytes=64)
+            return codes, scales
+
+        junk_w = const.tile([P, K], BF16, name="junk_w")
+        ss = const.tile([P, 2], F32, name="ss")
+        c2h = const.tile([P, 2], F32, name="c2h")
+        cw = const.tile([P, 2], F32, name="cw")
+        wnorm = const.tile([P, 2], F32, name="wnorm")
+        rinv = const.tile([P, 2], F32, name="rinv")
+        nb = const.tile([P, 2], F32, name="nb")
+        for h in range(2):
+            nc.scalar.activation(out=junk_w[:], in_=w_sb[:, h * K:(h + 1) * K], func=ACT.Square,
+                                 accum_out=ss[:, h:h + 1])
+        nc.scalar.activation(out=wnorm[:], in_=ss[:], func=ACT.Sqrt)
+
+        def words_transposed(src, name):
+            src_f = src[:].bitcast(F32)
+            tp = ps_t.tile([P, 2, N], F32, name=name + "_tp", tag="tb")
+            for h in range(2):
+                for u in range(2):
+                    nc.tensor.transpose(tp[:, u, h * P:(h + 1) * P],
+                                        src_f[:, h * 256 + u * P:h * 256 + (u + 1) * P], ident_f[:])
+            grp = const.tile([P, 4 * N], BF16, name=name + "_grp", align_bytes=64)
+            nc.scalar.copy(out=grp[:].bitcast(F32).rearrange("p (c u) -> p c u", u=2),
+                           in_=tp[:].rearrange("p u c -> p c u"))
+            return grp
+
+        w_grp = words_transposed(w_sb, "w")
+        c_grp = words_transposed(c_sb, "c")
+        for h in range(2):
+            nc.scalar.activation(out=junk_w[:], in_=c_sb[:, h * K:(h + 1) * K], func=ACT.Square,
+                                 scale=R, accum_out=c2h[:, h:h + 1])
+        w_codes, w_scales = quantised("w", N)
+        c_codes, c_scales = quantised("c", N)
+        wn_codes, wn_scales = quantised("wn", N)
+        prod = const.tile([P, 2 * K], F32, name="prod")
+        nc.gpsimd.tensor_tensor(out=prod[:], in0=c_sb[:], in1=w_sb[:], op=ALU.mult)
+
+        def late_prep():
+            nc.vector.quantize_mx(out=wn_codes[:].bitcast(FP8X4), scales=wn_scales[:], in_=wn_grp[:])
+            nc.vector.scalar_tensor_tensor(out=nb[:], in0=cw[:], scalar=-R, in1=rinv[:],
+                                           op0=ALU.mult, op1=ALU.mult)
+            nc.vector.reciprocal(out=is2[:], in_=is2[:])
+
+        st = {}
+
+        def ok(j):
+            return 0 <= j < NCH
+
+        def x2_rows(j, tiles):
+            if not ok(j):
+                return
+            for t in tiles:
+                junk = work.tile([P, K], BF16, name="junk", tag="junk")
+                nc.scalar.activation(out=junk[:], in_=x_sb[j][:, t * K:(t + 1) * K], func=ACT.Square,
+                                     scale=R, accum_out=x2h[:, j * TPC + t:j * TPC + t + 1])
+
+        def t1(j):
+            if not ok(j):
+                return
+            x_f = x_sb[j][:].bitcast(F32)
+            for b in range(2):
+                tp = ps_x.tile([P, 2, 2 * P], F32, name="xt", tag="xt")
+                for tt in range(2):
+                    for u in range(2):
+                        col = (2 * b + tt) * 256 + u * P
+                        nc.tensor.transpose(tp[:, u, tt * P:(tt + 1) * P], x_f[:, col:col + P], ident_f[:])
+                st[("xt", j, b)] = tp
+
+        def ev(j):
+            if not ok(j):
+                return
+            grp = work.tile([P, 4 * CW], BF16, name="grp", tag="grp", align_bytes=64)
+            g3 = grp[:].bitcast(F32).rearrange("p (c u) -> p c u", u=2)
+            for b in range(2):
+                nc.vector.tensor_copy(out=g3[:, b * 2 * P:(b + 1) * 2 * P, :],
+                                      in_=st[("xt", j, b)][:].rearrange("p u c -> p c u"))
+            st[("grp", j)] = grp
+
+        def quant(j):
+            if not ok(j):
+                return
+            codes = work.tile([P, CW], U32, name="xcodes", tag="xcodes", bufs=3, align_bytes=64)
+            scales = work.tile([P, CW], U8, name="xscales", tag="xscales", bufs=3, align_bytes=64)
+            nc.vector.quantize_mx(out=codes[:].bitcast(FP8X4), scales=scales[:], in_=st[("grp", j)][:])
+            st[("q", j)] = (codes, scales)
+
+        def m_a(j, b):
+            if not ok(j):
+                return
+            codes, scales = st[("q", j)]
+            acc = ps_a.tile([P, 2, N], F32, name="a", tag="a")
+            for tt in range(2):
+                cols = slice((2 * b + tt) * P, (2 * b + tt + 1) * P)
+                nc.tensor.matmul_mx(out=acc[:, tt, :], lhsT=codes[:, cols].bitcast(FP8X4),
+                                    lhsT_scale=scales[:, cols],
+                                    rhs=w_codes[:].bitcast(FP8X4), rhs_scale=w_scales[:],
+                                    start=True, stop=True)
+            st[("a", j, b)] = acc
+
+        def m_bc(j, h, nm):
+            if not ok(j):
+                return
+            codes, scales = st[("q", j)]
+            cd, sc = (wn_codes, wn_scales) if nm == "b" else (c_codes, c_scales)
+            cols = slice(h * P, (h + 1) * P)
+            acc = ps_bc.tile([P, CW], F32, name="bc", tag="bc")
+            nc.tensor.matmul_mx(out=acc[:], lhsT=cd[:, cols].bitcast(FP8X4), lhsT_scale=sc[:, cols],
+                                rhs=codes[:].bitcast(FP8X4), rhs_scale=scales[:], start=True, stop=True)
+            st[(nm, j, h)] = acc
+
+        def sq(j, h):
+            if not ok(j):
+                return
+            t2 = work.tile([P, CW], F32, name="t2", tag="t2")
+            nc.scalar.activation(out=t2[:], in_=st[("b", j, h)][:], func=ACT.Square,
+                                 bias=nb[:, h:h + 1], scale=R)
+            st[("t2", j, h)] = t2
+
+        def u_op(j, h):
+            if not ok(j):
+                return
+            u_sb = work.tile([P, CW], F32, name="u_sb", tag="u_sb", bufs=4)
+            nc.vector.scalar_tensor_tensor(out=u_sb[:], in0=st[("c", j, h)][:], scalar=c2h[:, h:h + 1],
+                                           in1=st[("t2", j, h)][:], op0=ALU.subtract, op1=ALU.add)
+            st[("u", j, h)] = u_sb
+
+        def pw_op(j, b):
+            if not ok(j):
+                return
+            if b == 0:
+                st[("pw", j)] = work.tile([P, TPC, N], F32, name="pw", tag="pw", bufs=3)
+            nc.vector.tensor_tensor(out=st[("pw", j)][:, 2 * b:2 * b + 2, :], in0=st[("a", j, b)][:],
+                                    in1=bias_b, op=ALU.add)
+
+        def t2_op(j):
+            if not ok(j):
+                return
+            for b in range(2):
+                tp = ps_t.tile([P, 2, N], F32, name="tb", tag="tb")
+                for tt in range(2):
+                    for h in range(2):
+                        t = 2 * b + tt
+                        nc.tensor.transpose(tp[:, tt, h * P:(h + 1) * P],
+                                            st[("u", j, h)][:, t * P:(t + 1) * P], ident_f[:])
+                st[("tb", j, b)] = tp
+
+        def w_op(j, b):
+            if not ok(j):
+                return
+            if b == 0:
+                st[("w", j)] = work.tile([P, TPC, N], F32, name="w_e", tag="w_e")
+                st[("om", j)] = work.tile([P, TPC, N], F32, name="om", tag="om")
+                st[("o", j)] = work.tile([P, TPC, N], F32, name="o_sb", tag="o_sb", bufs=3)
+            for tt in range(2):
+                t = 2 * b + tt
+                nc.vector.scalar_tensor_tensor(out=st[("w", j)][:, t, :], in0=st[("tb", j, b)][:, tt, :],
+                                               scalar=x2h[:, j * TPC + t:j * TPC + t + 1], in1=is2[:],
+                                               op0=ALU.subtract, op1=ALU.mult)
+
+        def ex_mul(j, b):
+            if not ok(j):
+                return
+            sl = slice(2 * b, 2 * b + 2)
+            nc.scalar.activation(out=st[("om", j)][:, sl, :], in_=st[("w", j)][:, sl, :], func=ACT.Exp)
+            eng = nc.vector if (LAST_MUL_ON_VECTOR and j == NCH - 1 and b == 1) else nc.gpsimd
+            eng.tensor_tensor(out=st[("o", j)][:, sl, :], in0=st[("pw", j)][:, sl, :],
+                              in1=st[("om", j)][:, sl, :], op=ALU.mult)
+            if j == NCH - 1:
+                nc.sync.dma_start(out=ov[:, j, b * 2 * N:(b + 1) * 2 * N],
+                                  in_=st[("o", j)][:, sl, :].rearrange("p t n -> p (t n)"))
+            elif b == 1:
+                nc.sync.dma_start(out=ov[:, j, :], in_=st[("o", j)][:].rearrange("p t n -> p (t n)"))
+
+        t1(0)
+        nc.vector.tensor_scalar_max(out=wnorm[:], in0=wnorm[:], scalar1=1e-12)
+        nc.vector.reciprocal(out=rinv[:], in_=wnorm[:])
+        wn = const.tile([P, 2 * K], BF16, name="wn")
+        for h in range(2):
+            nc.vector.tensor_scalar(
+                out=wn[:, h * K:(h + 1) * K].rearrange("n (u e p) -> n u e p", u=2, e=2),
+                in0=w_sb[:, h * K:(h + 1) * K].rearrange("n (u p e) -> n u e p", u=2, e=2),
+                scalar1=rinv[:, h:h + 1], scalar2=None, op0=ALU.mult)
+        wn_tp = ps_bc.tile([P, 4, N], BF16, name="wn_tp", tag="bc")
+        for h in range(2):
+            for t in range(4):
+                nc.tensor.transpose(wn_tp[:, t, h * P:(h + 1) * P],
+                                    wn[:, h * K + t * P:h * K + (t + 1) * P], ident_b[:])
+        bs_ps = ps_bc.tile([P, 2 * N], F32, name="bs_ps", tag="bc")
+        nc.tensor.matmul(bs_ps[:], lhsT=ones_b[:], rhs=vec[:], start=True, stop=True)
+        ev(0)
+        wn_grp = const.tile([P, 4 * N], BF16, name="wn_grp", align_bytes=64)
+        nc.scalar.copy(out=wn_grp[:].rearrange("p (c t) -> p c t", t=4),
+                       in_=wn_tp[:].rearrange("p t c -> p c t"))
+        for h in range(2):
+            nc.scalar.activation(out=junk_w[:], in_=prod[:, h * K:(h + 1) * K], func=ACT.Copy,
+                                 accum_out=cw[:, h:h + 1])
+        bias_sb = const.tile([P, N], F32, name="bias_sb")
+        nc.scalar.copy(out=bias_sb[:], in_=bs_ps[:, 0:N])
+        is2 = const.tile([P, N], F32, name="is2")
+        nc.scalar.activation(out=is2[:], in_=bs_ps[:, N:2 * N], func=ACT.Square, scale=R)
+        bias_b = bias_sb[:].unsqueeze(1).to_broadcast([P, 2, N])
+
+        t1(1)
+        nc.vector.quantize_mx(out=w_codes[:].bitcast(FP8X4), scales=w_scales[:], in_=w_grp[:])
+        nc.vector.quantize_mx(out=c_codes[:].bitcast(FP8X4), scales=c_scales[:], in_=c_grp[:])
+        quant(0)
+        late_prep()
+        x2_rows(0, [0, 1, 2, 3])
+
+        for i in range(-1, NCH):
+            t2_op(i)
+            ev(i + 2)
+            t1(i + 3)
+            w_op(i, 0)
+            ex_mul(i, 0)
+            x2_rows(i + 2, [0])
+            quant(i + 2)
+            w_op(i, 1)
+            m_a(i + 1, 0)
+            m_bc(i + 1, 0, "b")
+            m_bc(i + 1, 0, "c")
+            m_bc(i + 1, 1, "b")
+            sq(i + 1, 0)
+            pw_op(i + 1, 0)
+            m_a(i + 1, 1)
+            m_bc(i + 1, 1, "c")
+            sq(i + 1, 1)
+            ex_mul(i, 1)
+            u_op(i + 1, 0)
+            pw_op(i + 1, 1)
+            u_op(i + 1, 1)
+            x2_rows(i + 2, [1, 2, 3])

@@ -20,7 +20,6 @@ NCH = M // (P * TPC)
 CW = P * TPC
 R = math.sqrt(0.5)
 PINNED = True
-LAST_MUL_ON_VECTOR = True
 
 
 def tile_orthogonallyattenuatedlinear_t_kernel(tc, x, weights, bias, center, sigma, out):
@@ -30,7 +29,8 @@ def tile_orthogonallyattenuatedlinear_t_kernel(tc, x, weights, bias, center, sig
         xpool = ctx.enter_context(tc.tile_pool(name="xpool", bufs=1))
         work = ctx.enter_context(tc.tile_pool(name="work", bufs=2))
         ps_x = ctx.enter_context(tc.psum_pool(name="ps_x", bufs=2))
-        ps_bc = ctx.enter_context(tc.psum_pool(name="ps_bc", bufs=3))
+        ps_b = ctx.enter_context(tc.psum_pool(name="ps_b", bufs=2))
+        ps_c = ctx.enter_context(tc.psum_pool(name="ps_c", bufs=1))
         ps_a = ctx.enter_context(tc.psum_pool(name="ps_a", bufs=1))
         ps_t = ctx.enter_context(tc.psum_pool(name="ps_t", bufs=2))
         if PINNED:
@@ -141,7 +141,7 @@ def tile_orthogonallyattenuatedlinear_t_kernel(tc, x, weights, bias, center, sig
         def ev(j):
             if not ok(j):
                 return
-            grp = work.tile([P, 4 * CW], BF16, name="grp", tag="grp", align_bytes=64)
+            grp = work.tile([P, 4 * CW], BF16, name="grp", tag="grp", bufs=3, align_bytes=64)
             g3 = grp[:].bitcast(F32).rearrange("p (c u) -> p c u", u=2)
             for b in range(2):
                 nc.vector.tensor_copy(out=g3[:, b * 2 * P:(b + 1) * 2 * P, :],
@@ -151,8 +151,8 @@ def tile_orthogonallyattenuatedlinear_t_kernel(tc, x, weights, bias, center, sig
         def quant(j):
             if not ok(j):
                 return
-            codes = work.tile([P, CW], U32, name="xcodes", tag="xcodes", bufs=3, align_bytes=64)
-            scales = work.tile([P, CW], U8, name="xscales", tag="xscales", bufs=3, align_bytes=64)
+            codes = work.tile([P, CW], U32, name="xcodes", tag="xcodes", bufs=4, align_bytes=64)
+            scales = work.tile([P, CW], U8, name="xscales", tag="xscales", bufs=4, align_bytes=64)
             nc.vector.quantize_mx(out=codes[:].bitcast(FP8X4), scales=scales[:], in_=st[("grp", j)][:])
             st[("q", j)] = (codes, scales)
 
@@ -175,7 +175,8 @@ def tile_orthogonallyattenuatedlinear_t_kernel(tc, x, weights, bias, center, sig
             codes, scales = st[("q", j)]
             cd, sc = (wn_codes, wn_scales) if nm == "b" else (c_codes, c_scales)
             cols = slice(h * P, (h + 1) * P)
-            acc = ps_bc.tile([P, CW], F32, name="bc", tag="bc")
+            pool = ps_b if nm == "b" else ps_c
+            acc = pool.tile([P, CW], F32, name=nm, tag=nm)
             nc.tensor.matmul_mx(out=acc[:], lhsT=cd[:, cols].bitcast(FP8X4), lhsT_scale=sc[:, cols],
                                 rhs=codes[:].bitcast(FP8X4), rhs_scale=scales[:], start=True, stop=True)
             st[(nm, j, h)] = acc
@@ -183,7 +184,7 @@ def tile_orthogonallyattenuatedlinear_t_kernel(tc, x, weights, bias, center, sig
         def sq(j, h):
             if not ok(j):
                 return
-            t2 = work.tile([P, CW], F32, name="t2", tag="t2")
+            t2 = work.tile([P, CW], F32, name="t2", tag="t2", bufs=4)
             nc.scalar.activation(out=t2[:], in_=st[("b", j, h)][:], func=ACT.Square,
                                  bias=nb[:, h:h + 1], scale=R)
             st[("t2", j, h)] = t2
@@ -229,19 +230,16 @@ def tile_orthogonallyattenuatedlinear_t_kernel(tc, x, weights, bias, center, sig
                                                scalar=x2h[:, j * TPC + t:j * TPC + t + 1], in1=is2[:],
                                                op0=ALU.subtract, op1=ALU.mult)
 
-        def ex_mul(j, b):
+        def ex_mul(j, parts):
             if not ok(j):
                 return
-            sl = slice(2 * b, 2 * b + 2)
-            nc.scalar.activation(out=st[("om", j)][:, sl, :], in_=st[("w", j)][:, sl, :], func=ACT.Exp)
-            eng = nc.vector if (LAST_MUL_ON_VECTOR and j == NCH - 1 and b == 1) else nc.gpsimd
-            eng.tensor_tensor(out=st[("o", j)][:, sl, :], in0=st[("pw", j)][:, sl, :],
-                              in1=st[("om", j)][:, sl, :], op=ALU.mult)
-            if j == NCH - 1:
-                nc.sync.dma_start(out=ov[:, j, b * 2 * N:(b + 1) * 2 * N],
+            for t0, nt, eng in parts:
+                sl = slice(t0, t0 + nt)
+                nc.scalar.activation(out=st[("om", j)][:, sl, :], in_=st[("w", j)][:, sl, :], func=ACT.Exp)
+                eng.tensor_tensor(out=st[("o", j)][:, sl, :], in0=st[("pw", j)][:, sl, :],
+                                  in1=st[("om", j)][:, sl, :], op=ALU.mult)
+                nc.sync.dma_start(out=ov[:, j, t0 * N:(t0 + nt) * N],
                                   in_=st[("o", j)][:, sl, :].rearrange("p t n -> p (t n)"))
-            elif b == 1:
-                nc.sync.dma_start(out=ov[:, j, :], in_=st[("o", j)][:].rearrange("p t n -> p (t n)"))
 
         t1(0)
         nc.vector.tensor_scalar_max(out=wnorm[:], in0=wnorm[:], scalar1=1e-12)
@@ -252,12 +250,12 @@ def tile_orthogonallyattenuatedlinear_t_kernel(tc, x, weights, bias, center, sig
                 out=wn[:, h * K:(h + 1) * K].rearrange("n (u e p) -> n u e p", u=2, e=2),
                 in0=w_sb[:, h * K:(h + 1) * K].rearrange("n (u p e) -> n u e p", u=2, e=2),
                 scalar1=rinv[:, h:h + 1], scalar2=None, op0=ALU.mult)
-        wn_tp = ps_bc.tile([P, 4, N], BF16, name="wn_tp", tag="bc")
+        wn_tp = ps_b.tile([P, 4, N], BF16, name="wn_tp", tag="b")
         for h in range(2):
             for t in range(4):
                 nc.tensor.transpose(wn_tp[:, t, h * P:(h + 1) * P],
                                     wn[:, h * K + t * P:h * K + (t + 1) * P], ident_b[:])
-        bs_ps = ps_bc.tile([P, 2 * N], F32, name="bs_ps", tag="bc")
+        bs_ps = ps_b.tile([P, 2 * N], F32, name="bs_ps", tag="b")
         nc.tensor.matmul(bs_ps[:], lhsT=ones_b[:], rhs=vec[:], start=True, stop=True)
         ev(0)
         wn_grp = const.tile([P, 4 * N], BF16, name="wn_grp", align_bytes=64)
@@ -275,30 +273,36 @@ def tile_orthogonallyattenuatedlinear_t_kernel(tc, x, weights, bias, center, sig
         t1(1)
         nc.vector.quantize_mx(out=w_codes[:].bitcast(FP8X4), scales=w_scales[:], in_=w_grp[:])
         nc.vector.quantize_mx(out=c_codes[:].bitcast(FP8X4), scales=c_scales[:], in_=c_grp[:])
+        ev(1)
         quant(0)
         late_prep()
-        x2_rows(0, [0, 1, 2, 3])
 
-        for i in range(-1, NCH):
+        for i in range(-2, NCH):
+            last = i == NCH - 1
             t2_op(i)
-            ev(i + 2)
-            t1(i + 3)
-            w_op(i, 0)
-            ex_mul(i, 0)
-            x2_rows(i + 2, [0])
-            quant(i + 2)
-            w_op(i, 1)
-            m_a(i + 1, 0)
-            m_bc(i + 1, 0, "b")
-            m_bc(i + 1, 0, "c")
-            m_bc(i + 1, 1, "b")
-            sq(i + 1, 0)
-            pw_op(i + 1, 0)
-            m_a(i + 1, 1)
-            m_bc(i + 1, 1, "c")
-            sq(i + 1, 1)
-            ex_mul(i, 1)
+            t1(i + 4)
             u_op(i + 1, 0)
-            pw_op(i + 1, 1)
+            pw_op(i + 1, 0)
+            m_bc(i + 1, 1, "c")
+            m_a(i + 1, 1)
+            if i > -2:
+                x2_rows(i + 2, [0, 1, 2])
+            w_op(i, 0)
+            if last:
+                ex_mul(i, [(0, 2, nc.gpsimd)])
+            w_op(i, 1)
+            m_bc(i + 2, 0, "b")
+            m_bc(i + 2, 1, "b")
+            sq(i + 2, 0)
+            sq(i + 2, 1)
             u_op(i + 1, 1)
-            x2_rows(i + 2, [1, 2, 3])
+            pw_op(i + 1, 1)
+            m_bc(i + 2, 0, "c")
+            m_a(i + 2, 0)
+            if last:
+                ex_mul(i, [(2, 2, nc.vector)])
+            else:
+                ex_mul(i, [(0, 4, nc.gpsimd)])
+            ev(i + 4)
+            quant(i + 3)
+            x2_rows(i + 2, [3] if i > -2 else [0, 1, 2, 3])

@@ -52,7 +52,10 @@ def tile_orthogonallyattenuatedlinear_t_kernel(tc, x, weights, bias, center, sig
         x_sb = []
         for c in range(NCH):
             xt_c = xpool.tile([P, TPC * K], BF16, name="x%d" % c)
-            nc.sync.dma_start(out=xt_c[:], in_=xv[:, c, :])
+            pieces = 2 if c == 0 else 1
+            width = TPC * K // pieces
+            for s in range(pieces):
+                nc.sync.dma_start(out=xt_c[:, s * width:(s + 1) * width], in_=xv[:, c, s * width:(s + 1) * width])
             x_sb.append(xt_c)
 
         one1 = const.tile([P, 1], F32, name="one1")
@@ -79,10 +82,17 @@ def tile_orthogonallyattenuatedlinear_t_kernel(tc, x, weights, bias, center, sig
         wnorm = const.tile([P, 2], F32, name="wnorm")
         rinv = const.tile([P, 2], F32, name="rinv")
         nb = const.tile([P, 2], F32, name="nb")
-        for h in range(2):
-            nc.scalar.activation(out=junk_w[:], in_=w_sb[:, h * K:(h + 1) * K], func=ACT.Square,
-                                 accum_out=ss[:, h:h + 1])
-        nc.scalar.activation(out=wnorm[:], in_=ss[:], func=ACT.Sqrt)
+        w_codes, w_scales = quantised("w", N)
+        c_codes, c_scales = quantised("c", N)
+        wn_codes, wn_scales = quantised("wn", N)
+        w_grp = const.tile([P, 4 * N], BF16, name="w_grp", align_bytes=64)
+        c_grp = const.tile([P, 4 * N], BF16, name="c_grp", align_bytes=64)
+        wn_grp = const.tile([P, 4 * N], BF16, name="wn_grp", align_bytes=64)
+        wn = const.tile([P, 2 * K], BF16, name="wn")
+        prod = const.tile([P, 2, K], F32, name="prod")
+        bias_sb = const.tile([P, N], F32, name="bias_sb")
+        is2 = const.tile([P, N], F32, name="is2")
+        bias_b = bias_sb[:].unsqueeze(1).to_broadcast([P, 2, N])
 
         def words_transposed(src, name):
             src_f = src[:].bitcast(F32)
@@ -91,27 +101,11 @@ def tile_orthogonallyattenuatedlinear_t_kernel(tc, x, weights, bias, center, sig
                 for u in range(2):
                     nc.tensor.transpose(tp[:, u, h * P:(h + 1) * P],
                                         src_f[:, h * 256 + u * P:h * 256 + (u + 1) * P], ident_f[:])
-            grp = const.tile([P, 4 * N], BF16, name=name + "_grp", align_bytes=64)
-            nc.scalar.copy(out=grp[:].bitcast(F32).rearrange("p (c u) -> p c u", u=2),
-                           in_=tp[:].rearrange("p u c -> p c u"))
-            return grp
+            return tp
 
-        w_grp = words_transposed(w_sb, "w")
-        c_grp = words_transposed(c_sb, "c")
-        for h in range(2):
-            nc.scalar.activation(out=junk_w[:], in_=c_sb[:, h * K:(h + 1) * K], func=ACT.Square,
-                                 scale=R, accum_out=c2h[:, h:h + 1])
-        w_codes, w_scales = quantised("w", N)
-        c_codes, c_scales = quantised("c", N)
-        wn_codes, wn_scales = quantised("wn", N)
-        prod = const.tile([P, 2 * K], F32, name="prod")
-        nc.gpsimd.tensor_tensor(out=prod[:], in0=c_sb[:], in1=w_sb[:], op=ALU.mult)
-
-        def late_prep():
-            nc.vector.quantize_mx(out=wn_codes[:].bitcast(FP8X4), scales=wn_scales[:], in_=wn_grp[:])
-            nc.vector.scalar_tensor_tensor(out=nb[:], in0=cw[:], scalar=-R, in1=rinv[:],
-                                           op0=ALU.mult, op1=ALU.mult)
-            nc.vector.reciprocal(out=is2[:], in_=is2[:])
+        def words_out(tp, grp):
+            nc.vector.tensor_copy(out=grp[:].bitcast(F32).rearrange("p (c u) -> p c u", u=2),
+                                  in_=tp[:].rearrange("p u c -> p c u"))
 
         st = {}
 
@@ -241,15 +235,30 @@ def tile_orthogonallyattenuatedlinear_t_kernel(tc, x, weights, bias, center, sig
                 nc.sync.dma_start(out=ov[:, j, t0 * N:(t0 + nt) * N],
                                   in_=st[("o", j)][:, sl, :].rearrange("p t n -> p (t n)"))
 
+        nc.scalar.activation(out=junk_w[:], in_=w_sb[:, 0:K], func=ACT.Square, accum_out=ss[:, 0:1])
+        nc.scalar.activation(out=junk_w[:], in_=w_sb[:, K:2 * K], func=ACT.Square, accum_out=ss[:, 1:2])
+        nc.scalar.activation(out=wnorm[:], in_=ss[:], func=ACT.Sqrt)
         t1(0)
+        w_tp = words_transposed(w_sb, "w")
+        c_tp = words_transposed(c_sb, "c")
+        ev(0)
+        words_out(w_tp, w_grp)
         nc.vector.tensor_scalar_max(out=wnorm[:], in0=wnorm[:], scalar1=1e-12)
         nc.vector.reciprocal(out=rinv[:], in_=wnorm[:])
-        wn = const.tile([P, 2 * K], BF16, name="wn")
         for h in range(2):
             nc.vector.tensor_scalar(
                 out=wn[:, h * K:(h + 1) * K].rearrange("n (u e p) -> n u e p", u=2, e=2),
                 in0=w_sb[:, h * K:(h + 1) * K].rearrange("n (u p e) -> n u e p", u=2, e=2),
                 scalar1=rinv[:, h:h + 1], scalar2=None, op0=ALU.mult)
+        words_out(c_tp, c_grp)
+        for h in range(2):
+            nc.scalar.activation(out=junk_w[:], in_=c_sb[:, h * K:(h + 1) * K], func=ACT.Square,
+                                 scale=R, accum_out=c2h[:, h:h + 1])
+        nc.gpsimd.tensor_tensor(out=prod[:], in0=c_sb[:].rearrange("p (h k) -> p h k", h=2),
+                                in1=w_sb[:].rearrange("p (h k) -> p h k", h=2), op=ALU.mult)
+        for width in (256, 128, 64, 32, 16):
+            nc.gpsimd.tensor_tensor(out=prod[:, :, 0:width], in0=prod[:, :, 0:width],
+                                    in1=prod[:, :, width:2 * width], op=ALU.add)
         wn_tp = ps_b.tile([P, 4, N], BF16, name="wn_tp", tag="b")
         for h in range(2):
             for t in range(4):
@@ -257,25 +266,20 @@ def tile_orthogonallyattenuatedlinear_t_kernel(tc, x, weights, bias, center, sig
                                     wn[:, h * K + t * P:h * K + (t + 1) * P], ident_b[:])
         bs_ps = ps_b.tile([P, 2 * N], F32, name="bs_ps", tag="b")
         nc.tensor.matmul(bs_ps[:], lhsT=ones_b[:], rhs=vec[:], start=True, stop=True)
-        ev(0)
-        wn_grp = const.tile([P, 4 * N], BF16, name="wn_grp", align_bytes=64)
+        t1(1)
         nc.scalar.copy(out=wn_grp[:].rearrange("p (c t) -> p c t", t=4),
                        in_=wn_tp[:].rearrange("p t c -> p c t"))
-        for h in range(2):
-            nc.scalar.activation(out=junk_w[:], in_=prod[:, h * K:(h + 1) * K], func=ACT.Copy,
-                                 accum_out=cw[:, h:h + 1])
-        bias_sb = const.tile([P, N], F32, name="bias_sb")
         nc.scalar.copy(out=bias_sb[:], in_=bs_ps[:, 0:N])
-        is2 = const.tile([P, N], F32, name="is2")
         nc.scalar.activation(out=is2[:], in_=bs_ps[:, N:2 * N], func=ACT.Square, scale=R)
-        bias_b = bias_sb[:].unsqueeze(1).to_broadcast([P, 2, N])
-
-        t1(1)
         nc.vector.quantize_mx(out=w_codes[:].bitcast(FP8X4), scales=w_scales[:], in_=w_grp[:])
+        quant(0)
         nc.vector.quantize_mx(out=c_codes[:].bitcast(FP8X4), scales=c_scales[:], in_=c_grp[:])
         ev(1)
-        quant(0)
-        late_prep()
+        nc.vector.quantize_mx(out=wn_codes[:].bitcast(FP8X4), scales=wn_scales[:], in_=wn_grp[:])
+        nc.vector.tensor_reduce(out=cw[:], in_=prod[:, :, 0:16], axis=mybir.AxisListType.X, op=ALU.add)
+        nc.vector.scalar_tensor_tensor(out=nb[:], in0=cw[:], scalar=-R, in1=rinv[:],
+                                       op0=ALU.mult, op1=ALU.mult)
+        nc.vector.reciprocal(out=is2[:], in_=is2[:])
 
         for i in range(-2, NCH):
             last = i == NCH - 1
@@ -288,8 +292,6 @@ def tile_orthogonallyattenuatedlinear_t_kernel(tc, x, weights, bias, center, sig
             if i > -2:
                 x2_rows(i + 2, [0, 1, 2])
             w_op(i, 0)
-            if last:
-                ex_mul(i, [(0, 2, nc.gpsimd)])
             w_op(i, 1)
             m_bc(i + 2, 0, "b")
             m_bc(i + 2, 1, "b")
@@ -300,9 +302,9 @@ def tile_orthogonallyattenuatedlinear_t_kernel(tc, x, weights, bias, center, sig
             m_bc(i + 2, 0, "c")
             m_a(i + 2, 0)
             if last:
-                ex_mul(i, [(2, 2, nc.vector)])
+                ex_mul(i, [(t, 1, nc.vector) for t in range(TPC)])
             else:
-                ex_mul(i, [(0, 4, nc.gpsimd)])
+                ex_mul(i, [(0, TPC, nc.gpsimd)])
             ev(i + 4)
             quant(i + 3)
             x2_rows(i + 2, [3] if i > -2 else [0, 1, 2, 3])

@@ -1,5 +1,4 @@
 from contextlib import ExitStack
-import math
 
 import concourse.masks as masks
 import concourse.mybir as mybir
@@ -18,8 +17,7 @@ FLOPS = 3 * 2 * M * K * N
 TPC = 4
 NCH = M // (P * TPC)
 CW = P * TPC
-R = math.sqrt(0.5)
-PINNED = True
+NK = 6
 
 
 def tile_orthogonallyattenuatedlinear_t_kernel(tc, x, weights, bias, center, sigma, out):
@@ -33,8 +31,7 @@ def tile_orthogonallyattenuatedlinear_t_kernel(tc, x, weights, bias, center, sig
         ps_c = ctx.enter_context(tc.psum_pool(name="ps_c", bufs=1))
         ps_a = ctx.enter_context(tc.psum_pool(name="ps_a", bufs=1))
         ps_t = ctx.enter_context(tc.psum_pool(name="ps_t", bufs=2))
-        if PINNED:
-            ctx.enter_context(tc.manual_schedule())
+        ctx.enter_context(tc.manual_schedule())
 
         xv = x.rearrange("(p c t) k -> p c (t k)", c=NCH, t=TPC)
         ov = out.rearrange("(p c t) n -> p c (t n)", c=NCH, t=TPC)
@@ -43,32 +40,36 @@ def tile_orthogonallyattenuatedlinear_t_kernel(tc, x, weights, bias, center, sig
         c_sb = const.tile([P, 2 * K], BF16, name="c_sb")
         vec = const.tile([P, 2 * N], BF16, name="vec")
         nc.gpsimd.memset(vec[:], 0.0)
-        nc.scalar.dma_start(out=w_sb[:].rearrange("p (h k) -> p h k", h=2),
-                            in_=weights.rearrange("(h p) k -> p h k", h=2))
-        nc.scalar.dma_start(out=c_sb[:].rearrange("p (h k) -> p h k", h=2),
-                            in_=center.rearrange("(h p) k -> p h k", h=2))
-        nc.scalar.dma_start(out=vec[0:1, 0:N], in_=bias.unsqueeze(0))
-        nc.scalar.dma_start(out=vec[0:1, N:2 * N], in_=sigma.unsqueeze(0))
-        x_sb = []
-        for c in range(NCH):
-            xt_c = xpool.tile([P, TPC * K], BF16, name="x%d" % c)
-            pieces = 2 if c == 0 else 1
+        x_sb = [xpool.tile([P, TPC * K], BF16, name="x%d" % c) for c in range(NCH)]
+
+        def load_x(c, pieces):
             width = TPC * K // pieces
             for s in range(pieces):
-                nc.sync.dma_start(out=xt_c[:, s * width:(s + 1) * width], in_=xv[:, c, s * width:(s + 1) * width])
-            x_sb.append(xt_c)
+                nc.sync.dma_start(out=x_sb[c][:, s * width:(s + 1) * width], in_=xv[:, c, s * width:(s + 1) * width])
+
+        nc.sync.dma_start(out=w_sb[:].rearrange("p (h k) -> p h k", h=2),
+                          in_=weights.rearrange("(h p) k -> p h k", h=2))
+        load_x(0, 2)
+        nc.sync.dma_start(out=c_sb[:].rearrange("p (h k) -> p h k", h=2),
+                          in_=center.rearrange("(h p) k -> p h k", h=2))
+        nc.sync.dma_start(out=vec[0:1, 0:N], in_=bias.unsqueeze(0))
+        nc.sync.dma_start(out=vec[0:1, N:2 * N], in_=sigma.unsqueeze(0))
+        for c in range(1, NCH):
+            load_x(c, 1)
 
         one1 = const.tile([P, 1], F32, name="one1")
         nc.vector.memset(one1[:], 1.0)
         dummy = const.tile([P, 1], F32, name="dummy")
-        nc.scalar.activation(out=dummy[:], in_=one1[:], func=ACT.Sqrt)
+        nc.scalar.activation(out=dummy[:], in_=one1[:], func=ACT.Exp)
+        mhalf = const.tile([P, 2], F32, name="mhalf")
+        nc.vector.memset(mhalf[:], -0.5)
         ident_f = const.tile([P, P], F32, name="ident_f")
         masks.make_identity(nc, ident_f[:])
         ident_b = const.tile([P, P], BF16, name="ident_b")
-        masks.make_identity(nc, ident_b[:])
+        nc.vector.tensor_copy(out=ident_b[:], in_=ident_f[:])
         ones_b = const.tile([P, P], BF16, name="ones_b")
         nc.vector.memset(ones_b[:], 1.0)
-        x2h = const.tile([P, NCH * TPC], F32, name="x2h")
+        x2 = const.tile([P, NCH * TPC], F32, name="x2")
 
         def quantised(name, width):
             codes = const.tile([P, width], U32, name=name + "_codes", align_bytes=64)
@@ -76,10 +77,10 @@ def tile_orthogonallyattenuatedlinear_t_kernel(tc, x, weights, bias, center, sig
             return codes, scales
 
         junk_w = const.tile([P, K], BF16, name="junk_w")
+        junk_v = const.tile([P, K], BF16, name="junk_v")
         ss = const.tile([P, 2], F32, name="ss")
-        c2h = const.tile([P, 2], F32, name="c2h")
+        c2 = const.tile([P, 2], F32, name="c2")
         cw = const.tile([P, 2], F32, name="cw")
-        wnorm = const.tile([P, 2], F32, name="wnorm")
         rinv = const.tile([P, 2], F32, name="rinv")
         nb = const.tile([P, 2], F32, name="nb")
         w_codes, w_scales = quantised("w", N)
@@ -89,9 +90,17 @@ def tile_orthogonallyattenuatedlinear_t_kernel(tc, x, weights, bias, center, sig
         c_grp = const.tile([P, 4 * N], BF16, name="c_grp", align_bytes=64)
         wn_grp = const.tile([P, 4 * N], BF16, name="wn_grp", align_bytes=64)
         wn = const.tile([P, 2 * K], BF16, name="wn")
-        prod = const.tile([P, 2, K], F32, name="prod")
         bias_sb = const.tile([P, N], F32, name="bias_sb")
-        is2 = const.tile([P, N], F32, name="is2")
+        rs = const.tile([P, 2], F32, name="rs")
+        is2x2 = const.tile([P, 2], F32, name="is2x2")
+        coef = const.tile([P, 2, 2], F32, name="coef")
+        res = const.tile([P, 2, 2], F32, name="res")
+        ph = const.tile([P, 2, 2], BF16, name="ph")
+        pm = const.tile([P, 2, 2], BF16, name="pm")
+        pl = const.tile([P, 2, 2], BF16, name="pl")
+        zr = const.tile([P, 2, TPC * P], BF16, name="zr")
+        rk = const.tile([P, TPC, N], BF16, name="rk")
+        z = []
         bias_b = bias_sb[:].unsqueeze(1).to_broadcast([P, 2, N])
 
         def words_transposed(src, name):
@@ -103,8 +112,8 @@ def tile_orthogonallyattenuatedlinear_t_kernel(tc, x, weights, bias, center, sig
                                         src_f[:, h * 256 + u * P:h * 256 + (u + 1) * P], ident_f[:])
             return tp
 
-        def words_out(tp, grp):
-            nc.vector.tensor_copy(out=grp[:].bitcast(F32).rearrange("p (c u) -> p c u", u=2),
+        def words_out(tp, grp, copy):
+            copy(out=grp[:].bitcast(F32).rearrange("p (c u) -> p c u", u=2),
                                   in_=tp[:].rearrange("p u c -> p c u"))
 
         st = {}
@@ -118,13 +127,13 @@ def tile_orthogonallyattenuatedlinear_t_kernel(tc, x, weights, bias, center, sig
             for t in tiles:
                 junk = work.tile([P, K], BF16, name="junk", tag="junk")
                 nc.scalar.activation(out=junk[:], in_=x_sb[j][:, t * K:(t + 1) * K], func=ACT.Square,
-                                     scale=R, accum_out=x2h[:, j * TPC + t:j * TPC + t + 1])
+                                     accum_out=x2[:, j * TPC + t:j * TPC + t + 1])
 
-        def t1(j):
+        def t1(j, halves=(0, 1)):
             if not ok(j):
                 return
             x_f = x_sb[j][:].bitcast(F32)
-            for b in range(2):
+            for b in halves:
                 tp = ps_x.tile([P, 2, 2 * P], F32, name="xt", tag="xt")
                 for tt in range(2):
                     for u in range(2):
@@ -132,15 +141,15 @@ def tile_orthogonallyattenuatedlinear_t_kernel(tc, x, weights, bias, center, sig
                         nc.tensor.transpose(tp[:, u, tt * P:(tt + 1) * P], x_f[:, col:col + P], ident_f[:])
                 st[("xt", j, b)] = tp
 
-        def ev(j):
+        def ev(j, halves=(0, 1)):
             if not ok(j):
                 return
-            grp = work.tile([P, 4 * CW], BF16, name="grp", tag="grp", bufs=3, align_bytes=64)
-            g3 = grp[:].bitcast(F32).rearrange("p (c u) -> p c u", u=2)
-            for b in range(2):
+            for b in halves:
+                if b == 0:
+                    st[("grp", j)] = work.tile([P, 4 * CW], BF16, name="grp", tag="grp", bufs=3, align_bytes=64)
+                g3 = st[("grp", j)][:].bitcast(F32).rearrange("p (c u) -> p c u", u=2)
                 nc.vector.tensor_copy(out=g3[:, b * 2 * P:(b + 1) * 2 * P, :],
                                       in_=st[("xt", j, b)][:].rearrange("p u c -> p c u"))
-            st[("grp", j)] = grp
 
         def quant(j):
             if not ok(j):
@@ -180,15 +189,15 @@ def tile_orthogonallyattenuatedlinear_t_kernel(tc, x, weights, bias, center, sig
                 return
             t2 = work.tile([P, CW], F32, name="t2", tag="t2", bufs=4)
             nc.scalar.activation(out=t2[:], in_=st[("b", j, h)][:], func=ACT.Square,
-                                 bias=nb[:, h:h + 1], scale=R)
+                                 bias=nb[:, h:h + 1], scale=rs[:, h:h + 1])
             st[("t2", j, h)] = t2
 
         def u_op(j, h):
             if not ok(j):
                 return
             u_sb = work.tile([P, CW], F32, name="u_sb", tag="u_sb", bufs=4)
-            nc.vector.scalar_tensor_tensor(out=u_sb[:], in0=st[("c", j, h)][:], scalar=c2h[:, h:h + 1],
-                                           in1=st[("t2", j, h)][:], op0=ALU.subtract, op1=ALU.add)
+            nc.vector.scalar_tensor_tensor(out=u_sb[:], in0=st[("c", j, h)][:], scalar=is2x2[:, h:h + 1],
+                                           in1=st[("t2", j, h)][:], op0=ALU.mult, op1=ALU.add)
             st[("u", j, h)] = u_sb
 
         def pw_op(j, b):
@@ -199,112 +208,170 @@ def tile_orthogonallyattenuatedlinear_t_kernel(tc, x, weights, bias, center, sig
             nc.vector.tensor_tensor(out=st[("pw", j)][:, 2 * b:2 * b + 2, :], in0=st[("a", j, b)][:],
                                     in1=bias_b, op=ALU.add)
 
-        def t2_op(j):
+        def z_split(j):
             if not ok(j):
                 return
-            for b in range(2):
+            zt = z[j % 3][:].rearrange("p (k t) -> p k t", t=TPC)
+            xc = x2[:, j * TPC:(j + 1) * TPC]
+            r1 = work.tile([P, TPC], F32, name="r1", tag="r1")
+            nc.gpsimd.tensor_copy(out=zt[:, 0:3, :], in_=xc.unsqueeze(1).to_broadcast([P, 3, TPC]))
+            nc.gpsimd.tensor_tensor(out=r1[:], in0=xc, in1=zt[:, 0, :], op=ALU.subtract)
+            nc.gpsimd.tensor_copy(out=zt[:, 3:5, :], in_=r1[:].unsqueeze(1).to_broadcast([P, 2, TPC]))
+            nc.gpsimd.tensor_tensor(out=zt[:, 5, :], in0=r1[:], in1=zt[:, 3, :], op=ALU.subtract)
+
+        def z_t(j):
+            if not ok(j):
+                return
+            tp = ps_c.tile([P, P], BF16, name="zt", tag="c")
+            nc.tensor.transpose(tp[:], z[j % 3][:], ident_b[:])
+            zs = work.tile([P, P], BF16, name="zs", tag="zs", bufs=3)
+            nc.vector.tensor_copy(out=zs[:], in_=tp[:])
+            st[("zs", j)] = zs
+
+        def t2_op(j, halves=(0, 1)):
+            if not ok(j):
+                return
+            for b in halves:
                 tp = ps_t.tile([P, 2, N], F32, name="tb", tag="tb")
                 for tt in range(2):
+                    t = 2 * b + tt
+                    nc.tensor.matmul(tp[:, tt, :], lhsT=st[("zs", j)][:], rhs=rk[:, t, :], start=True, stop=False)
                     for h in range(2):
-                        t = 2 * b + tt
-                        nc.tensor.transpose(tp[:, tt, h * P:(h + 1) * P],
-                                            st[("u", j, h)][:, t * P:(t + 1) * P], ident_f[:])
+                        nc.tensor.matmul(tp[:, tt, h * P:(h + 1) * P], lhsT=st[("u", j, h)][:, t * P:(t + 1) * P],
+                                         rhs=ident_f[:], is_transpose=True, start=False, stop=h == 1)
                 st[("tb", j, b)] = tp
 
-        def w_op(j, b):
+        def ex(j, t0, nt):
             if not ok(j):
                 return
-            if b == 0:
-                st[("w", j)] = work.tile([P, TPC, N], F32, name="w_e", tag="w_e")
+            if t0 == 0:
                 st[("om", j)] = work.tile([P, TPC, N], F32, name="om", tag="om")
-                st[("o", j)] = work.tile([P, TPC, N], F32, name="o_sb", tag="o_sb", bufs=3)
-            for tt in range(2):
-                t = 2 * b + tt
-                nc.vector.scalar_tensor_tensor(out=st[("w", j)][:, t, :], in0=st[("tb", j, b)][:, tt, :],
-                                               scalar=x2h[:, j * TPC + t:j * TPC + t + 1], in1=is2[:],
-                                               op0=ALU.subtract, op1=ALU.mult)
+            nc.scalar.activation(out=st[("om", j)][:, t0:t0 + nt, :],
+                                 in_=st[("tb", j, t0 // 2)][:, t0 % 2:t0 % 2 + nt, :], func=ACT.Exp)
 
-        def ex_mul(j, parts):
+        def mul(j, t0, nt, eng):
             if not ok(j):
                 return
-            for t0, nt, eng in parts:
-                sl = slice(t0, t0 + nt)
-                nc.scalar.activation(out=st[("om", j)][:, sl, :], in_=st[("w", j)][:, sl, :], func=ACT.Exp)
-                eng.tensor_tensor(out=st[("o", j)][:, sl, :], in0=st[("pw", j)][:, sl, :],
-                                  in1=st[("om", j)][:, sl, :], op=ALU.mult)
-                nc.sync.dma_start(out=ov[:, j, t0 * N:(t0 + nt) * N],
-                                  in_=st[("o", j)][:, sl, :].rearrange("p t n -> p (t n)"))
+            if t0 == 0:
+                st[("o", j)] = work.tile([P, TPC, N], F32, name="o_sb", tag="o_sb", bufs=3)
+            sl = slice(t0, t0 + nt)
+            eng.tensor_tensor(out=st[("o", j)][:, sl, :], in0=st[("pw", j)][:, sl, :],
+                              in1=st[("om", j)][:, sl, :], op=ALU.mult)
+            nc.sync.dma_start(out=ov[:, j, t0 * N:(t0 + nt) * N],
+                              in_=st[("o", j)][:, sl, :].rearrange("p t n -> p (t n)"))
 
-        nc.scalar.activation(out=junk_w[:], in_=w_sb[:, 0:K], func=ACT.Square, accum_out=ss[:, 0:1])
-        nc.scalar.activation(out=junk_w[:], in_=w_sb[:, K:2 * K], func=ACT.Square, accum_out=ss[:, 1:2])
-        nc.scalar.activation(out=wnorm[:], in_=ss[:], func=ACT.Sqrt)
+        def w_half(t, h):
+            return t[:, h * K:(h + 1) * K]
+
+        nc.scalar.activation(out=junk_w[:], in_=w_half(w_sb, 0), func=ACT.Square, accum_out=ss[:, 0:1])
+        nc.vector.scalar_tensor_tensor(out=junk_v[:], in0=w_half(w_sb, 1), scalar=1.0, in1=w_half(w_sb, 1),
+                                       op0=ALU.mult, op1=ALU.mult, accum_out=ss[:, 1:2])
+        nc.vector.tensor_scalar_max(out=ss[:], in0=ss[:], scalar1=1e-24)
+        nc.gpsimd.tensor_tensor(out=rinv[:], in0=ss[:], in1=mhalf[:], op=ALU.pow)
+        nc.gpsimd.memset(zr[:], 0.0)
+        for i in range(3):
+            z_i = const.tile([P, P], BF16, name="z%d" % i)
+            nc.gpsimd.memset(z_i[:], 0.0)
+            nc.gpsimd.memset(z_i[:, NK * TPC:NK * TPC + 3], 1.0)
+            z.append(z_i)
         t1(0)
         w_tp = words_transposed(w_sb, "w")
         c_tp = words_transposed(c_sb, "c")
+        x2_rows(0, [0, 1, 2, 3])
+        words_out(c_tp, c_grp, nc.scalar.copy)
         ev(0)
-        words_out(w_tp, w_grp)
-        nc.vector.tensor_scalar_max(out=wnorm[:], in0=wnorm[:], scalar1=1e-12)
-        nc.vector.reciprocal(out=rinv[:], in_=wnorm[:])
         for h in range(2):
             nc.vector.tensor_scalar(
-                out=wn[:, h * K:(h + 1) * K].rearrange("n (u e p) -> n u e p", u=2, e=2),
-                in0=w_sb[:, h * K:(h + 1) * K].rearrange("n (u p e) -> n u e p", u=2, e=2),
+                out=w_half(wn, h).rearrange("n (u e p) -> n u e p", u=2, e=2),
+                in0=w_half(w_sb, h).rearrange("n (u p e) -> n u e p", u=2, e=2),
                 scalar1=rinv[:, h:h + 1], scalar2=None, op0=ALU.mult)
-        words_out(c_tp, c_grp)
-        for h in range(2):
-            nc.scalar.activation(out=junk_w[:], in_=c_sb[:, h * K:(h + 1) * K], func=ACT.Square,
-                                 scale=R, accum_out=c2h[:, h:h + 1])
-        nc.gpsimd.tensor_tensor(out=prod[:], in0=c_sb[:].rearrange("p (h k) -> p h k", h=2),
-                                in1=w_sb[:].rearrange("p (h k) -> p h k", h=2), op=ALU.mult)
-        for width in (256, 128, 64, 32, 16):
-            nc.gpsimd.tensor_tensor(out=prod[:, :, 0:width], in0=prod[:, :, 0:width],
-                                    in1=prod[:, :, width:2 * width], op=ALU.add)
         wn_tp = ps_b.tile([P, 4, N], BF16, name="wn_tp", tag="b")
         for h in range(2):
             for t in range(4):
                 nc.tensor.transpose(wn_tp[:, t, h * P:(h + 1) * P],
                                     wn[:, h * K + t * P:h * K + (t + 1) * P], ident_b[:])
-        bs_ps = ps_b.tile([P, 2 * N], F32, name="bs_ps", tag="b")
-        nc.tensor.matmul(bs_ps[:], lhsT=ones_b[:], rhs=vec[:], start=True, stop=True)
+        bs_ps = ps_b.tile([P, N], F32, name="bs_ps", tag="b")
+        nc.tensor.matmul(bs_ps[:], lhsT=ones_b[:], rhs=vec[:, 0:N], start=True, stop=True)
+        sg_ps = ps_a.tile([P, 2, P], BF16, name="sg_ps", tag="a")
+        for h in range(2):
+            nc.tensor.transpose(sg_ps[:, h, :], vec[:, N + h * P:N + (h + 1) * P], ident_b[:])
         t1(1)
-        nc.scalar.copy(out=wn_grp[:].rearrange("p (c t) -> p c t", t=4),
-                       in_=wn_tp[:].rearrange("p t c -> p c t"))
-        nc.scalar.copy(out=bias_sb[:], in_=bs_ps[:, 0:N])
-        nc.scalar.activation(out=is2[:], in_=bs_ps[:, N:2 * N], func=ACT.Square, scale=R)
-        nc.vector.quantize_mx(out=w_codes[:].bitcast(FP8X4), scales=w_scales[:], in_=w_grp[:])
+        for h in range(2):
+            nc.vector.scalar_tensor_tensor(out=junk_v[:], in0=w_half(c_sb, h), scalar=rinv[:, h:h + 1],
+                                           in1=w_half(w_sb, h), op0=ALU.mult, op1=ALU.mult,
+                                           accum_out=cw[:, h:h + 1])
+            nc.scalar.activation(out=junk_w[:], in_=w_half(c_sb, h), func=ACT.Square, accum_out=c2[:, h:h + 1])
+        x2_rows(1, [0, 1, 2, 3])
+        nc.scalar.copy(out=bias_sb[:], in_=bs_ps[:])
+        nc.vector.tensor_copy(out=wn_grp[:].rearrange("p (c t) -> p c t", t=4),
+                              in_=wn_tp[:].rearrange("p t c -> p c t"))
         quant(0)
-        nc.vector.quantize_mx(out=c_codes[:].bitcast(FP8X4), scales=c_scales[:], in_=c_grp[:])
-        ev(1)
+        nc.vector.reciprocal(out=rs[:], in_=sg_ps[:, :, 0])
         nc.vector.quantize_mx(out=wn_codes[:].bitcast(FP8X4), scales=wn_scales[:], in_=wn_grp[:])
-        nc.vector.tensor_reduce(out=cw[:], in_=prod[:, :, 0:16], axis=mybir.AxisListType.X, op=ALU.add)
-        nc.vector.scalar_tensor_tensor(out=nb[:], in0=cw[:], scalar=-R, in1=rinv[:],
+        nc.vector.scalar_tensor_tensor(out=nb[:], in0=cw[:], scalar=-1.0, in1=rs[:], op0=ALU.mult, op1=ALU.mult)
+        nc.vector.scalar_tensor_tensor(out=coef[:, 0, :], in0=rs[:], scalar=-1.0, in1=rs[:],
                                        op0=ALU.mult, op1=ALU.mult)
-        nc.vector.reciprocal(out=is2[:], in_=is2[:])
+        nc.vector.scalar_tensor_tensor(out=is2x2[:], in0=rs[:], scalar=2.0, in1=rs[:], op0=ALU.mult, op1=ALU.mult)
+        words_out(w_tp, w_grp, nc.vector.tensor_copy)
+        nc.vector.quantize_mx(out=c_codes[:].bitcast(FP8X4), scales=c_scales[:], in_=c_grp[:])
+        nc.vector.quantize_mx(out=w_codes[:].bitcast(FP8X4), scales=w_scales[:], in_=w_grp[:])
+        ev(1)
+        t1(2)
+        z_split(0)
+        z_split(1)
+
+        nc.gpsimd.tensor_tensor(out=coef[:, 1, :], in0=coef[:, 0, :], in1=c2[:], op=ALU.mult)
+        nc.gpsimd.tensor_copy(out=ph[:], in_=coef[:])
+        nc.gpsimd.tensor_tensor(out=res[:], in0=coef[:], in1=ph[:], op=ALU.subtract)
+        nc.gpsimd.tensor_copy(out=pm[:], in_=res[:])
+        nc.gpsimd.tensor_tensor(out=pl[:], in0=res[:], in1=pm[:], op=ALU.subtract)
+        for k, piece in enumerate([ph, pm, pl, ph, pm, ph]):
+            nc.gpsimd.tensor_copy(out=zr[:, :, k * TPC:k * TPC + (TPC - 1) * (P + 1) + 1:P + 1],
+                                  in_=piece[:, 0, :].unsqueeze(2).to_broadcast([P, 2, TPC]))
+        for k, piece in enumerate([ph, pm, pl]):
+            c0 = NK * TPC + k
+            nc.gpsimd.tensor_copy(out=zr[:, :, c0:c0 + (TPC - 1) * P + 1:P],
+                                  in_=piece[:, 1, :].unsqueeze(2).to_broadcast([P, 2, TPC]))
 
         for i in range(-2, NCH):
             last = i == NCH - 1
-            t2_op(i)
-            t1(i + 4)
+            t2_op(i, [0])
             u_op(i + 1, 0)
-            pw_op(i + 1, 0)
             m_bc(i + 1, 1, "c")
+            x2_rows(i + 4, [0])
+            if not last:
+                ex(i, 0, 2)
+            pw_op(i + 1, 0)
             m_a(i + 1, 1)
-            if i > -2:
-                x2_rows(i + 2, [0, 1, 2])
-            w_op(i, 0)
-            w_op(i, 1)
+            t2_op(i, [1])
+            ev(i + 4, [0])
+            u_op(i + 1, 1)
+            x2_rows(i + 4, [1, 2])
+            if last:
+                for t in range(TPC):
+                    ex(i, t, 1)
+                    mul(i, t, 1, nc.vector)
+            else:
+                ex(i, 2, 2)
+                mul(i, 0, TPC, nc.gpsimd)
+            pw_op(i + 1, 1)
+            z_t(i + 2)
             m_bc(i + 2, 0, "b")
             m_bc(i + 2, 1, "b")
             sq(i + 2, 0)
             sq(i + 2, 1)
-            u_op(i + 1, 1)
-            pw_op(i + 1, 1)
+            t1(i + 5, [0])
             m_bc(i + 2, 0, "c")
             m_a(i + 2, 0)
-            if last:
-                ex_mul(i, [(t, 1, nc.vector) for t in range(TPC)])
-            else:
-                ex_mul(i, [(0, TPC, nc.gpsimd)])
-            ev(i + 4)
+            ev(i + 4, [1])
+            t1(i + 5, [1])
             quant(i + 3)
-            x2_rows(i + 2, [3] if i > -2 else [0, 1, 2, 3])
+            x2_rows(i + 4, [3])
+            z_split(i + 4)
+            if i == -2:
+                rk_ps = ps_t.tile([P, TPC, N], BF16, name="rk_ps", tag="tb")
+                for t in range(TPC):
+                    for h in range(2):
+                        nc.tensor.transpose(rk_ps[:, t, h * P:(h + 1) * P], zr[:, h, t * P:(t + 1) * P], ident_b[:])
+            if i == -1:
+                nc.vector.tensor_copy(out=rk[:], in_=rk_ps[:])

@@ -39,7 +39,9 @@ def tile_orthogonallyattenuatedlinear_t_kernel(tc, x, weights, bias, center, sig
         w_sb = const.tile([P, 2 * K], BF16, name="w_sb")
         c_sb = const.tile([P, 2 * K], BF16, name="c_sb")
         vec = const.tile([P, 2 * N], BF16, name="vec")
-        nc.gpsimd.memset(vec[:], 0.0)
+        one1 = const.tile([P, 1], F32, name="one1")
+        nc.vector.memset(one1[:], 1.0)
+        nc.vector.memset(vec[:], 0.0)
         x_sb = [xpool.tile([P, TPC * K], BF16, name="x%d" % c) for c in range(NCH)]
 
         def load_x(c, pieces):
@@ -50,15 +52,13 @@ def tile_orthogonallyattenuatedlinear_t_kernel(tc, x, weights, bias, center, sig
         nc.sync.dma_start(out=w_sb[:].rearrange("p (h k) -> p h k", h=2),
                           in_=weights.rearrange("(h p) k -> p h k", h=2))
         load_x(0, 2)
-        nc.sync.dma_start(out=c_sb[:].rearrange("p (h k) -> p h k", h=2),
-                          in_=center.rearrange("(h p) k -> p h k", h=2))
         nc.sync.dma_start(out=vec[0:1, 0:N], in_=bias.unsqueeze(0))
         nc.sync.dma_start(out=vec[0:1, N:2 * N], in_=sigma.unsqueeze(0))
+        nc.sync.dma_start(out=c_sb[:].rearrange("p (h k) -> p h k", h=2),
+                          in_=center.rearrange("(h p) k -> p h k", h=2))
         for c in range(1, NCH):
             load_x(c, 1)
 
-        one1 = const.tile([P, 1], F32, name="one1")
-        nc.vector.memset(one1[:], 1.0)
         dummy = const.tile([P, 1], F32, name="dummy")
         nc.scalar.activation(out=dummy[:], in_=one1[:], func=ACT.Exp)
         mhalf = const.tile([P, 2], F32, name="mhalf")
@@ -103,9 +103,9 @@ def tile_orthogonallyattenuatedlinear_t_kernel(tc, x, weights, bias, center, sig
         z = []
         bias_b = bias_sb[:].unsqueeze(1).to_broadcast([P, 2, N])
 
-        def words_transposed(src, name):
+        def words_transposed(src, name, pool=ps_t, tag="tb"):
             src_f = src[:].bitcast(F32)
-            tp = ps_t.tile([P, 2, N], F32, name=name + "_tp", tag="tb")
+            tp = pool.tile([P, 2, N], F32, name=name + "_tp", tag=tag)
             for h in range(2):
                 for u in range(2):
                     nc.tensor.transpose(tp[:, u, h * P:(h + 1) * P],
@@ -125,9 +125,19 @@ def tile_orthogonallyattenuatedlinear_t_kernel(tc, x, weights, bias, center, sig
             if not ok(j):
                 return
             for t in tiles:
+                if ("x2", j, t) in st:
+                    continue
+                st[("x2", j, t)] = True
                 junk = work.tile([P, K], BF16, name="junk", tag="junk")
                 nc.scalar.activation(out=junk[:], in_=x_sb[j][:, t * K:(t + 1) * K], func=ACT.Square,
                                      accum_out=x2[:, j * TPC + t:j * TPC + t + 1])
+
+        def x2_vec(j, t):
+            if not ok(j):
+                return
+            xt = x_sb[j][:, t * K:(t + 1) * K]
+            nc.vector.scalar_tensor_tensor(out=junk_v[:], in0=xt, scalar=1.0, in1=xt, op0=ALU.mult, op1=ALU.mult,
+                                           accum_out=x2[:, j * TPC + t:j * TPC + t + 1])
 
         def t1(j, halves=(0, 1)):
             if not ok(j):
@@ -163,7 +173,8 @@ def tile_orthogonallyattenuatedlinear_t_kernel(tc, x, weights, bias, center, sig
             if not ok(j):
                 return
             codes, scales = st[("q", j)]
-            acc = ps_a.tile([P, 2, N], F32, name="a", tag="a")
+            pool, tag = (ps_x, "xt") if j == NCH - 1 and b == 1 else (ps_a, "a")
+            acc = pool.tile([P, 2, N], F32, name="a", tag=tag)
             for tt in range(2):
                 cols = slice((2 * b + tt) * P, (2 * b + tt + 1) * P)
                 nc.tensor.matmul_mx(out=acc[:, tt, :], lhsT=codes[:, cols].bitcast(FP8X4),
@@ -173,13 +184,13 @@ def tile_orthogonallyattenuatedlinear_t_kernel(tc, x, weights, bias, center, sig
             st[("a", j, b)] = acc
 
         def m_bc(j, h, nm):
-            if not ok(j):
+            if not ok(j) or (nm, j, h) in st:
                 return
             codes, scales = st[("q", j)]
             cd, sc = (wn_codes, wn_scales) if nm == "b" else (c_codes, c_scales)
             cols = slice(h * P, (h + 1) * P)
-            pool = ps_b if nm == "b" else ps_c
-            acc = pool.tile([P, CW], F32, name=nm, tag=nm)
+            pool, tag = (ps_b, "b") if nm == "b" or (j == NCH - 1 and h == 1) else (ps_c, "c")
+            acc = pool.tile([P, CW], F32, name=nm, tag=tag)
             nc.tensor.matmul_mx(out=acc[:], lhsT=cd[:, cols].bitcast(FP8X4), lhsT_scale=sc[:, cols],
                                 rhs=codes[:].bitcast(FP8X4), rhs_scale=scales[:], start=True, stop=True)
             st[(nm, j, h)] = acc
@@ -209,6 +220,9 @@ def tile_orthogonallyattenuatedlinear_t_kernel(tc, x, weights, bias, center, sig
                                     in1=bias_b, op=ALU.add)
 
         def z_split(j):
+            if ("z", j) in st:
+                return
+            st[("z", j)] = True
             if not ok(j):
                 return
             zt = z[j % 3][:].rearrange("p (k t) -> p k t", t=TPC)
@@ -222,7 +236,7 @@ def tile_orthogonallyattenuatedlinear_t_kernel(tc, x, weights, bias, center, sig
         def z_t(j):
             if not ok(j):
                 return
-            tp = ps_c.tile([P, P], BF16, name="zt", tag="c")
+            tp = ps_a.tile([P, P], BF16, name="zt", tag="a")
             nc.tensor.transpose(tp[:], z[j % 3][:], ident_b[:])
             zs = work.tile([P, P], BF16, name="zs", tag="zs", bufs=3)
             nc.vector.tensor_copy(out=zs[:], in_=tp[:])
@@ -264,9 +278,8 @@ def tile_orthogonallyattenuatedlinear_t_kernel(tc, x, weights, bias, center, sig
             return t[:, h * K:(h + 1) * K]
 
         nc.scalar.activation(out=junk_w[:], in_=w_half(w_sb, 0), func=ACT.Square, accum_out=ss[:, 0:1])
-        nc.vector.scalar_tensor_tensor(out=junk_v[:], in0=w_half(w_sb, 1), scalar=1.0, in1=w_half(w_sb, 1),
-                                       op0=ALU.mult, op1=ALU.mult, accum_out=ss[:, 1:2])
-        nc.vector.tensor_scalar_max(out=ss[:], in0=ss[:], scalar1=1e-24)
+        nc.scalar.activation(out=junk_w[:], in_=w_half(w_sb, 1), func=ACT.Square, accum_out=ss[:, 1:2])
+        nc.gpsimd.tensor_scalar_max(out=ss[:], in0=ss[:], scalar1=1e-24)
         nc.gpsimd.tensor_tensor(out=rinv[:], in0=ss[:], in1=mhalf[:], op=ALU.pow)
         nc.gpsimd.memset(zr[:], 0.0)
         for i in range(3):
@@ -275,51 +288,44 @@ def tile_orthogonallyattenuatedlinear_t_kernel(tc, x, weights, bias, center, sig
             nc.gpsimd.memset(z_i[:, NK * TPC:NK * TPC + 3], 1.0)
             z.append(z_i)
         t1(0)
-        w_tp = words_transposed(w_sb, "w")
-        c_tp = words_transposed(c_sb, "c")
-        x2_rows(0, [0, 1, 2, 3])
-        words_out(c_tp, c_grp, nc.scalar.copy)
-        ev(0)
-        for h in range(2):
-            nc.vector.tensor_scalar(
-                out=w_half(wn, h).rearrange("n (u e p) -> n u e p", u=2, e=2),
-                in0=w_half(w_sb, h).rearrange("n (u p e) -> n u e p", u=2, e=2),
-                scalar1=rinv[:, h:h + 1], scalar2=None, op0=ALU.mult)
-        wn_tp = ps_b.tile([P, 4, N], BF16, name="wn_tp", tag="b")
-        for h in range(2):
-            for t in range(4):
-                nc.tensor.transpose(wn_tp[:, t, h * P:(h + 1) * P],
-                                    wn[:, h * K + t * P:h * K + (t + 1) * P], ident_b[:])
-        bs_ps = ps_b.tile([P, N], F32, name="bs_ps", tag="b")
-        nc.tensor.matmul(bs_ps[:], lhsT=ones_b[:], rhs=vec[:, 0:N], start=True, stop=True)
         sg_ps = ps_a.tile([P, 2, P], BF16, name="sg_ps", tag="a")
         for h in range(2):
             nc.tensor.transpose(sg_ps[:, h, :], vec[:, N + h * P:N + (h + 1) * P], ident_b[:])
+        c_tp = words_transposed(c_sb, "c")
+        w_tp = words_transposed(w_sb, "w")
+        x2_rows(0, [0, 1])
+        for h in range(2):
+            nc.scalar.activation(out=junk_w[:], in_=w_half(c_sb, h), func=ACT.Square, accum_out=c2[:, h:h + 1])
+        words_out(c_tp, c_grp, nc.scalar.copy)
+        x2_rows(0, [2, 3])
+        ev(0)
+        for h in range(2):
+            nc.vector.tensor_scalar(out=w_half(wn, h), in0=w_half(w_sb, h), scalar1=rinv[:, h:h + 1], scalar2=None,
+                                    op0=ALU.mult)
+        nc.vector.reciprocal(out=rs[:], in_=sg_ps[:, :, 0])
+        wn_tp = words_transposed(wn, "wn", ps_b, "b")
+        nc.vector.scalar_tensor_tensor(out=coef[:, 0, :], in0=rs[:], scalar=-1.0, in1=rs[:],
+                                       op0=ALU.mult, op1=ALU.mult)
+        bs_ps = ps_b.tile([P, N], F32, name="bs_ps", tag="b")
+        nc.tensor.matmul(bs_ps[:], lhsT=ones_b[:], rhs=vec[:, 0:N], start=True, stop=True)
         t1(1)
+        nc.scalar.copy(out=bias_sb[:], in_=bs_ps[:])
+        words_out(wn_tp, wn_grp, nc.vector.tensor_copy)
+        quant(0)
         for h in range(2):
             nc.vector.scalar_tensor_tensor(out=junk_v[:], in0=w_half(c_sb, h), scalar=rinv[:, h:h + 1],
                                            in1=w_half(w_sb, h), op0=ALU.mult, op1=ALU.mult,
                                            accum_out=cw[:, h:h + 1])
-            nc.scalar.activation(out=junk_w[:], in_=w_half(c_sb, h), func=ACT.Square, accum_out=c2[:, h:h + 1])
-        x2_rows(1, [0, 1, 2, 3])
-        nc.scalar.copy(out=bias_sb[:], in_=bs_ps[:])
-        nc.vector.tensor_copy(out=wn_grp[:].rearrange("p (c t) -> p c t", t=4),
-                              in_=wn_tp[:].rearrange("p t c -> p c t"))
-        quant(0)
-        nc.vector.reciprocal(out=rs[:], in_=sg_ps[:, :, 0])
         nc.vector.quantize_mx(out=wn_codes[:].bitcast(FP8X4), scales=wn_scales[:], in_=wn_grp[:])
-        nc.vector.scalar_tensor_tensor(out=nb[:], in0=cw[:], scalar=-1.0, in1=rs[:], op0=ALU.mult, op1=ALU.mult)
-        nc.vector.scalar_tensor_tensor(out=coef[:, 0, :], in0=rs[:], scalar=-1.0, in1=rs[:],
-                                       op0=ALU.mult, op1=ALU.mult)
         nc.vector.scalar_tensor_tensor(out=is2x2[:], in0=rs[:], scalar=2.0, in1=rs[:], op0=ALU.mult, op1=ALU.mult)
+        nc.vector.scalar_tensor_tensor(out=nb[:], in0=cw[:], scalar=-1.0, in1=rs[:], op0=ALU.mult, op1=ALU.mult)
         words_out(w_tp, w_grp, nc.vector.tensor_copy)
         nc.vector.quantize_mx(out=c_codes[:].bitcast(FP8X4), scales=c_scales[:], in_=c_grp[:])
         nc.vector.quantize_mx(out=w_codes[:].bitcast(FP8X4), scales=w_scales[:], in_=w_grp[:])
-        ev(1)
-        t1(2)
-        z_split(0)
-        z_split(1)
+        m_bc(0, 0, "b")
+        m_bc(0, 1, "b")
 
+        z_split(0)
         nc.gpsimd.tensor_tensor(out=coef[:, 1, :], in0=coef[:, 0, :], in1=c2[:], op=ALU.mult)
         nc.gpsimd.tensor_copy(out=ph[:], in_=coef[:])
         nc.gpsimd.tensor_tensor(out=res[:], in0=coef[:], in1=ph[:], op=ALU.subtract)
@@ -333,45 +339,48 @@ def tile_orthogonallyattenuatedlinear_t_kernel(tc, x, weights, bias, center, sig
             nc.gpsimd.tensor_copy(out=zr[:, :, c0:c0 + (TPC - 1) * P + 1:P],
                                   in_=piece[:, 1, :].unsqueeze(2).to_broadcast([P, 2, TPC]))
 
-        for i in range(-2, NCH):
-            last = i == NCH - 1
-            t2_op(i, [0])
-            u_op(i + 1, 0)
-            m_bc(i + 1, 1, "c")
-            x2_rows(i + 4, [0])
-            if not last:
-                ex(i, 0, 2)
-            pw_op(i + 1, 0)
-            m_a(i + 1, 1)
-            t2_op(i, [1])
-            ev(i + 4, [0])
-            u_op(i + 1, 1)
-            x2_rows(i + 4, [1, 2])
-            if last:
-                for t in range(TPC):
-                    ex(i, t, 1)
-                    mul(i, t, 1, nc.vector)
+        for j in range(-1, NCH):
+            m_bc(j + 1, 0, "b")
+            m_bc(j + 1, 1, "b")
+            u_op(j, 0)
+            m_bc(j, 1, "c")
+            x2_rows(j + 2, [0])
+            sq(j + 1, 0)
+            sq(j + 1, 1)
+            if j < NCH - 1:
+                pw_op(j, 0)
+            m_a(j, 1)
+            ev(j + 2, [0])
+            u_op(j, 1)
+            t1(j + 3, [0])
+            ev(j + 2, [1])
+            x2_rows(j + 2, [1, 2] if j % 2 == 0 else [1, 2, 3])
+            t2_op(j, [0])
+            if j == NCH - 1:
+                pw_op(j, 0)
+            pw_op(j, 1)
+            if j < NCH - 2:
+                ex(j, 0, 2)
+                t2_op(j, [1])
+                ex(j, 2, 2)
             else:
-                ex(i, 2, 2)
-                mul(i, 0, TPC, nc.gpsimd)
-            pw_op(i + 1, 1)
-            z_t(i + 2)
-            m_bc(i + 2, 0, "b")
-            m_bc(i + 2, 1, "b")
-            sq(i + 2, 0)
-            sq(i + 2, 1)
-            t1(i + 5, [0])
-            m_bc(i + 2, 0, "c")
-            m_a(i + 2, 0)
-            ev(i + 4, [1])
-            t1(i + 5, [1])
-            quant(i + 3)
-            x2_rows(i + 4, [3])
-            z_split(i + 4)
-            if i == -2:
+                t2_op(j, [1])
+                for t in range(TPC):
+                    ex(j, t, 1)
+                    mul(j, t, 1, nc.vector)
+            if j % 2 == 0:
+                x2_vec(j + 2, 3)
+            z_t(j + 1)
+            m_bc(j + 1, 0, "c")
+            m_a(j + 1, 0)
+            t1(j + 3, [1])
+            quant(j + 2)
+            z_split(j + 2)
+            if j < NCH - 2:
+                mul(j, 0, TPC, nc.gpsimd)
+            if j == -1:
                 rk_ps = ps_t.tile([P, TPC, N], BF16, name="rk_ps", tag="tb")
                 for t in range(TPC):
                     for h in range(2):
                         nc.tensor.transpose(rk_ps[:, t, h * P:(h + 1) * P], zr[:, h, t * P:(t + 1) * P], ident_b[:])
-            if i == -1:
-                nc.vector.tensor_copy(out=rk[:], in_=rk_ps[:])
+                nc.scalar.copy(out=rk[:], in_=rk_ps[:])

@@ -236,24 +236,32 @@ def tile_orthogonallyattenuatedlinear_t_kernel(tc, x, weights, bias, center, sig
         def z_t(j):
             if not ok(j):
                 return
-            tp = ps_a.tile([P, P], BF16, name="zt", tag="a")
+            tp = ps_c.tile([P, P], BF16, name="zt", tag="c")
             nc.tensor.transpose(tp[:], z[j % 3][:], ident_b[:])
-            zs = work.tile([P, P], BF16, name="zs", tag="zs", bufs=3)
-            nc.vector.tensor_copy(out=zs[:], in_=tp[:])
-            st[("zs", j)] = zs
+            st[("zt", j)] = tp
 
-        def t2_op(j, halves=(0, 1)):
+        def z_out(j):
             if not ok(j):
                 return
-            for b in halves:
+            zs = work.tile([P, P], BF16, name="zs", tag="zs", bufs=3)
+            nc.vector.tensor_copy(out=zs[:], in_=st[("zt", j)][:])
+            st[("zs", j)] = zs
+
+        def t2_op(j):
+            if not ok(j):
+                return
+            tbs = []
+            for b in range(2):
                 tp = ps_t.tile([P, 2, N], F32, name="tb", tag="tb")
+                nc.tensor.matmul(tp[:], lhsT=st[("zs", j)][:], rhs=rk[:, 2 * b:2 * b + 2, :], start=True, stop=False)
+                tbs.append(tp)
+            for b in range(2):
                 for tt in range(2):
-                    t = 2 * b + tt
-                    nc.tensor.matmul(tp[:, tt, :], lhsT=st[("zs", j)][:], rhs=rk[:, t, :], start=True, stop=False)
                     for h in range(2):
-                        nc.tensor.matmul(tp[:, tt, h * P:(h + 1) * P], lhsT=st[("u", j, h)][:, t * P:(t + 1) * P],
-                                         rhs=ident_f[:], is_transpose=True, start=False, stop=h == 1)
-                st[("tb", j, b)] = tp
+                        t = 2 * b + tt
+                        nc.tensor.matmul(tbs[b][:, tt, h * P:(h + 1) * P], lhsT=st[("u", j, h)][:, t * P:(t + 1) * P],
+                                         rhs=ident_f[:], is_transpose=True, start=False, stop=tt == 1 and h == 1)
+                st[("tb", j, b)] = tbs[b]
 
         def ex(j, t0, nt):
             if not ok(j):
@@ -340,41 +348,40 @@ def tile_orthogonallyattenuatedlinear_t_kernel(tc, x, weights, bias, center, sig
                                   in_=piece[:, 1, :].unsqueeze(2).to_broadcast([P, 2, TPC]))
 
         for j in range(-1, NCH):
-            m_bc(j + 1, 0, "b")
-            m_bc(j + 1, 1, "b")
+            last = j == NCH - 1
             u_op(j, 0)
             m_bc(j, 1, "c")
-            x2_rows(j + 2, [0])
             sq(j + 1, 0)
             sq(j + 1, 1)
-            if j < NCH - 1:
+            if not last:
                 pw_op(j, 0)
             m_a(j, 1)
             ev(j + 2, [0])
             u_op(j, 1)
             t1(j + 3, [0])
+            z_t(j + 1)
+            t2_op(j)
             ev(j + 2, [1])
-            x2_rows(j + 2, [1, 2] if j % 2 == 0 else [1, 2, 3])
-            t2_op(j, [0])
-            if j == NCH - 1:
+            t1(j + 3, [1])
+            x2_rows(j + 2, [0, 1, 2] if j % 2 == 0 else [0, 1, 2, 3])
+            if last:
                 pw_op(j, 0)
             pw_op(j, 1)
+            z_out(j + 1)
             if j < NCH - 2:
                 ex(j, 0, 2)
-                t2_op(j, [1])
                 ex(j, 2, 2)
             else:
-                t2_op(j, [1])
                 for t in range(TPC):
                     ex(j, t, 1)
                     mul(j, t, 1, nc.vector)
             if j % 2 == 0:
                 x2_vec(j + 2, 3)
-            z_t(j + 1)
             m_bc(j + 1, 0, "c")
             m_a(j + 1, 0)
-            t1(j + 3, [1])
             quant(j + 2)
+            m_bc(j + 2, 0, "b")
+            m_bc(j + 2, 1, "b")
             z_split(j + 2)
             if j < NCH - 2:
                 mul(j, 0, TPC, nc.gpsimd)

@@ -77,6 +77,7 @@ def tile_orthogonallyattenuatedlinear_t_kernel(tc, x, weights, bias, center, sig
             return codes, scales
 
         junk_w = const.tile([P, K], BF16, name="junk_w")
+        junk_c = const.tile([P, P], F32, name="junk_c")
         junk_v = const.tile([P, K], BF16, name="junk_v")
         ss = const.tile([P, 2], F32, name="ss")
         c2 = const.tile([P, 2], F32, name="c2")
@@ -169,11 +170,11 @@ def tile_orthogonallyattenuatedlinear_t_kernel(tc, x, weights, bias, center, sig
             nc.vector.quantize_mx(out=codes[:].bitcast(FP8X4), scales=scales[:], in_=st[("grp", j)][:])
             st[("q", j)] = (codes, scales)
 
-        def m_a(j, b):
+        def m_a(j, b, bank=None):
             if not ok(j):
                 return
             codes, scales = st[("q", j)]
-            pool, tag = (ps_x, "xt") if j == NCH - 1 and b == 1 else (ps_a, "a")
+            pool, tag = bank or (ps_a, "a")
             acc = pool.tile([P, 2, N], F32, name="a", tag=tag)
             for tt in range(2):
                 cols = slice((2 * b + tt) * P, (2 * b + tt + 1) * P)
@@ -183,13 +184,13 @@ def tile_orthogonallyattenuatedlinear_t_kernel(tc, x, weights, bias, center, sig
                                     start=True, stop=True)
             st[("a", j, b)] = acc
 
-        def m_bc(j, h, nm):
+        def m_bc(j, h, nm, bank=None):
             if not ok(j) or (nm, j, h) in st:
                 return
             codes, scales = st[("q", j)]
             cd, sc = (wn_codes, wn_scales) if nm == "b" else (c_codes, c_scales)
             cols = slice(h * P, (h + 1) * P)
-            pool, tag = (ps_b, "b") if nm == "b" or (j == NCH - 1 and h == 1) else (ps_c, "c")
+            pool, tag = bank or ((ps_b, "b") if nm == "b" else (ps_c, "c"))
             acc = pool.tile([P, CW], F32, name=nm, tag=tag)
             nc.tensor.matmul_mx(out=acc[:], lhsT=cd[:, cols].bitcast(FP8X4), lhsT_scale=sc[:, cols],
                                 rhs=codes[:].bitcast(FP8X4), rhs_scale=scales[:], start=True, stop=True)
@@ -236,7 +237,7 @@ def tile_orthogonallyattenuatedlinear_t_kernel(tc, x, weights, bias, center, sig
         def z_t(j):
             if not ok(j):
                 return
-            tp = ps_c.tile([P, P], BF16, name="zt", tag="c")
+            tp = ps_b.tile([P, P], BF16, name="zt", tag="b")
             nc.tensor.transpose(tp[:], z[j % 3][:], ident_b[:])
             st[("zt", j)] = tp
 
@@ -301,9 +302,9 @@ def tile_orthogonallyattenuatedlinear_t_kernel(tc, x, weights, bias, center, sig
             nc.tensor.transpose(sg_ps[:, h, :], vec[:, N + h * P:N + (h + 1) * P], ident_b[:])
         c_tp = words_transposed(c_sb, "c")
         w_tp = words_transposed(w_sb, "w")
-        x2_rows(0, [0, 1])
         for h in range(2):
             nc.scalar.activation(out=junk_w[:], in_=w_half(c_sb, h), func=ACT.Square, accum_out=c2[:, h:h + 1])
+        x2_rows(0, [0, 1])
         words_out(c_tp, c_grp, nc.scalar.copy)
         x2_rows(0, [2, 3])
         ev(0)
@@ -318,22 +319,25 @@ def tile_orthogonallyattenuatedlinear_t_kernel(tc, x, weights, bias, center, sig
         nc.tensor.matmul(bs_ps[:], lhsT=ones_b[:], rhs=vec[:, 0:N], start=True, stop=True)
         t1(1)
         nc.scalar.copy(out=bias_sb[:], in_=bs_ps[:])
+        words_out(w_tp, w_grp, nc.vector.tensor_copy)
+        cw_ps = ps_c.tile([P, 2, P], F32, name="cw_ps", tag="c")
+        c4 = c_grp[:].rearrange("p (c t) -> p c t", t=4)
+        w4 = w_grp[:].rearrange("p (c t) -> p c t", t=4)
+        for h in range(2):
+            for t in range(4):
+                nc.tensor.matmul(cw_ps[:, h, :], lhsT=c4[:, h * P:(h + 1) * P, t], rhs=w4[:, h * P:(h + 1) * P, t],
+                                 start=t == 0, stop=t == 3)
         words_out(wn_tp, wn_grp, nc.vector.tensor_copy)
         quant(0)
         for h in range(2):
-            nc.vector.scalar_tensor_tensor(out=junk_v[:], in0=w_half(c_sb, h), scalar=rinv[:, h:h + 1],
-                                           in1=w_half(w_sb, h), op0=ALU.mult, op1=ALU.mult,
-                                           accum_out=cw[:, h:h + 1])
+            nc.vector.scalar_tensor_tensor(out=junk_c[:], in0=cw_ps[:, h, :], scalar=rinv[:, h:h + 1], in1=ident_f[:],
+                                           op0=ALU.mult, op1=ALU.mult, accum_out=cw[:, h:h + 1])
         nc.vector.quantize_mx(out=wn_codes[:].bitcast(FP8X4), scales=wn_scales[:], in_=wn_grp[:])
         nc.vector.scalar_tensor_tensor(out=is2x2[:], in0=rs[:], scalar=2.0, in1=rs[:], op0=ALU.mult, op1=ALU.mult)
         nc.vector.scalar_tensor_tensor(out=nb[:], in0=cw[:], scalar=-1.0, in1=rs[:], op0=ALU.mult, op1=ALU.mult)
-        words_out(w_tp, w_grp, nc.vector.tensor_copy)
         nc.vector.quantize_mx(out=c_codes[:].bitcast(FP8X4), scales=c_scales[:], in_=c_grp[:])
         nc.vector.quantize_mx(out=w_codes[:].bitcast(FP8X4), scales=w_scales[:], in_=w_grp[:])
-        m_bc(0, 0, "b")
-        m_bc(0, 1, "b")
 
-        z_split(0)
         nc.gpsimd.tensor_tensor(out=coef[:, 1, :], in0=coef[:, 0, :], in1=c2[:], op=ALU.mult)
         nc.gpsimd.tensor_copy(out=ph[:], in_=coef[:])
         nc.gpsimd.tensor_tensor(out=res[:], in0=coef[:], in1=ph[:], op=ALU.subtract)
@@ -346,48 +350,70 @@ def tile_orthogonallyattenuatedlinear_t_kernel(tc, x, weights, bias, center, sig
             c0 = NK * TPC + k
             nc.gpsimd.tensor_copy(out=zr[:, :, c0:c0 + (TPC - 1) * P + 1:P],
                                   in_=piece[:, 1, :].unsqueeze(2).to_broadcast([P, 2, TPC]))
+        z_split(0)
+        x2_rows(1, [0, 1])
+        rk_ps = ps_t.tile([P, TPC, N], BF16, name="rk_ps", tag="tb")
+        for t in range(TPC):
+            for h in range(2):
+                nc.tensor.transpose(rk_ps[:, t, h * P:(h + 1) * P], zr[:, h, t * P:(t + 1) * P], ident_b[:])
+        nc.scalar.copy(out=rk[:], in_=rk_ps[:])
+        m_bc(0, 0, "b")
+        m_bc(0, 1, "b")
 
-        for j in range(-1, NCH):
-            last = j == NCH - 1
+        for j in range(-1, NCH - 2):
+            ev(j + 2, [0])
             u_op(j, 0)
             m_bc(j, 1, "c")
+            x2_rows(j + 2, [0])
             sq(j + 1, 0)
             sq(j + 1, 1)
-            if not last:
-                pw_op(j, 0)
+            pw_op(j, 0)
             m_a(j, 1)
-            ev(j + 2, [0])
+            ev(j + 2, [1])
             u_op(j, 1)
-            t1(j + 3, [0])
+            t1(j + 3)
             z_t(j + 1)
             t2_op(j)
-            ev(j + 2, [1])
-            t1(j + 3, [1])
-            x2_rows(j + 2, [0, 1, 2] if j % 2 == 0 else [0, 1, 2, 3])
-            if last:
-                pw_op(j, 0)
+            x2_rows(j + 2, [1, 2, 3])
             pw_op(j, 1)
-            z_out(j + 1)
-            if j < NCH - 2:
-                ex(j, 0, 2)
-                ex(j, 2, 2)
-            else:
-                for t in range(TPC):
-                    ex(j, t, 1)
-                    mul(j, t, 1, nc.vector)
-            if j % 2 == 0:
+            ex(j, 0, 2)
+            ex(j, 2, 2)
+            if False:
                 x2_vec(j + 2, 3)
             m_bc(j + 1, 0, "c")
             m_a(j + 1, 0)
             quant(j + 2)
+            z_out(j + 1)
             m_bc(j + 2, 0, "b")
             m_bc(j + 2, 1, "b")
             z_split(j + 2)
-            if j < NCH - 2:
-                mul(j, 0, TPC, nc.gpsimd)
-            if j == -1:
-                rk_ps = ps_t.tile([P, TPC, N], BF16, name="rk_ps", tag="tb")
-                for t in range(TPC):
-                    for h in range(2):
-                        nc.tensor.transpose(rk_ps[:, t, h * P:(h + 1) * P], zr[:, h, t * P:(t + 1) * P], ident_b[:])
-                nc.scalar.copy(out=rk[:], in_=rk_ps[:])
+            mul(j, 0, TPC, nc.gpsimd)
+
+        i, j = NCH - 2, NCH - 1
+        spare = (ps_x, "xt")
+        m_bc(i, 1, "c", spare)
+        m_a(i, 1, spare)
+        sq(j, 0)
+        sq(j, 1)
+        u_op(i, 0)
+        m_bc(j, 0, "c")
+        pw_op(i, 0)
+        m_a(j, 0)
+        u_op(i, 1)
+        m_bc(j, 1, "c", spare)
+        z_t(j)
+        t2_op(i)
+        ex(i, 0, 2)
+        ex(i, 2, 2)
+        u_op(j, 0)
+        z_out(j)
+        pw_op(i, 1)
+        mul(i, 0, TPC, nc.gpsimd)
+        u_op(j, 1)
+        m_a(j, 1, spare)
+        t2_op(j)
+        pw_op(j, 0)
+        pw_op(j, 1)
+        for t in range(TPC):
+            ex(j, t, 1)
+            mul(j, t, 1, nc.vector)

@@ -101,7 +101,13 @@ def tile_orthogonallyattenuatedlinear_t_kernel(tc, x, weights, bias, center, sig
         pl = const.tile([P, 2, 2], BF16, name="pl")
         zr = const.tile([P, 2, TPC * P], BF16, name="zr")
         rk = const.tile([P, TPC, N], BF16, name="rk")
+        nc.vector.memset(zr[:], 0.0)
         z = []
+        for i in range(3):
+            z_i = const.tile([P, P], BF16, name="z%d" % i)
+            nc.gpsimd.memset(z_i[:], 0.0)
+            nc.gpsimd.memset(z_i[:, NK * TPC:NK * TPC + 3], 1.0)
+            z.append(z_i)
         bias_b = bias_sb[:].unsqueeze(1).to_broadcast([P, 2, N])
 
         def words_transposed(src, name, pool=ps_t, tag="tb"):
@@ -248,12 +254,13 @@ def tile_orthogonallyattenuatedlinear_t_kernel(tc, x, weights, bias, center, sig
             nc.vector.tensor_copy(out=zs[:], in_=st[("zt", j)][:])
             st[("zs", j)] = zs
 
-        def t2_op(j):
+        def t2_op(j, bank=None):
             if not ok(j):
                 return
             tbs = []
             for b in range(2):
-                tp = ps_t.tile([P, 2, N], F32, name="tb", tag="tb")
+                pool, tag = bank or (ps_t, "tb")
+                tp = pool.tile([P, 2, N], F32, name="tb", tag=tag)
                 nc.tensor.matmul(tp[:], lhsT=st[("zs", j)][:], rhs=rk[:, 2 * b:2 * b + 2, :], start=True, stop=False)
                 tbs.append(tp)
             for b in range(2):
@@ -290,12 +297,6 @@ def tile_orthogonallyattenuatedlinear_t_kernel(tc, x, weights, bias, center, sig
         nc.scalar.activation(out=junk_w[:], in_=w_half(w_sb, 1), func=ACT.Square, accum_out=ss[:, 1:2])
         nc.gpsimd.tensor_scalar_max(out=ss[:], in0=ss[:], scalar1=1e-24)
         nc.gpsimd.tensor_tensor(out=rinv[:], in0=ss[:], in1=mhalf[:], op=ALU.pow)
-        nc.gpsimd.memset(zr[:], 0.0)
-        for i in range(3):
-            z_i = const.tile([P, P], BF16, name="z%d" % i)
-            nc.gpsimd.memset(z_i[:], 0.0)
-            nc.gpsimd.memset(z_i[:, NK * TPC:NK * TPC + 3], 1.0)
-            z.append(z_i)
         t1(0)
         sg_ps = ps_a.tile([P, 2, P], BF16, name="sg_ps", tag="a")
         for h in range(2):
@@ -308,18 +309,18 @@ def tile_orthogonallyattenuatedlinear_t_kernel(tc, x, weights, bias, center, sig
         words_out(c_tp, c_grp, nc.scalar.copy)
         x2_rows(0, [2, 3])
         ev(0)
+        nc.vector.reciprocal(out=rs[:], in_=sg_ps[:, :, 0])
+        nc.vector.scalar_tensor_tensor(out=coef[:, 0, :], in0=rs[:], scalar=-1.0, in1=rs[:],
+                                       op0=ALU.mult, op1=ALU.mult)
+        words_out(w_tp, w_grp, nc.vector.tensor_copy)
         for h in range(2):
             nc.vector.tensor_scalar(out=w_half(wn, h), in0=w_half(w_sb, h), scalar1=rinv[:, h:h + 1], scalar2=None,
                                     op0=ALU.mult)
-        nc.vector.reciprocal(out=rs[:], in_=sg_ps[:, :, 0])
         wn_tp = words_transposed(wn, "wn", ps_b, "b")
-        nc.vector.scalar_tensor_tensor(out=coef[:, 0, :], in0=rs[:], scalar=-1.0, in1=rs[:],
-                                       op0=ALU.mult, op1=ALU.mult)
         bs_ps = ps_b.tile([P, N], F32, name="bs_ps", tag="b")
         nc.tensor.matmul(bs_ps[:], lhsT=ones_b[:], rhs=vec[:, 0:N], start=True, stop=True)
         t1(1)
         nc.scalar.copy(out=bias_sb[:], in_=bs_ps[:])
-        words_out(w_tp, w_grp, nc.vector.tensor_copy)
         cw_ps = ps_c.tile([P, 2, P], F32, name="cw_ps", tag="c")
         c4 = c_grp[:].rearrange("p (c t) -> p c t", t=4)
         w4 = w_grp[:].rearrange("p (c t) -> p c t", t=4)
@@ -374,11 +375,11 @@ def tile_orthogonallyattenuatedlinear_t_kernel(tc, x, weights, bias, center, sig
             t1(j + 3)
             z_t(j + 1)
             t2_op(j)
-            x2_rows(j + 2, [1, 2, 3])
+            x2_rows(j + 2, [1, 2] if j in (0, 4) else [1, 2, 3])
             pw_op(j, 1)
             ex(j, 0, 2)
             ex(j, 2, 2)
-            if False:
+            if j in (0, 4):
                 x2_vec(j + 2, 3)
             m_bc(j + 1, 0, "c")
             m_a(j + 1, 0)
@@ -408,12 +409,13 @@ def tile_orthogonallyattenuatedlinear_t_kernel(tc, x, weights, bias, center, sig
         u_op(j, 0)
         z_out(j)
         pw_op(i, 1)
-        mul(i, 0, TPC, nc.gpsimd)
+        mul(i, 0, 2, nc.gpsimd)
         u_op(j, 1)
         m_a(j, 1, spare)
-        t2_op(j)
+        t2_op(j, (ps_b, "b"))
         pw_op(j, 0)
         pw_op(j, 1)
+        mul(i, 2, 2, nc.vector)
         for t in range(TPC):
             ex(j, t, 1)
             mul(j, t, 1, nc.vector)

@@ -49,8 +49,8 @@ def tile_orthogonallyattenuatedlinear_t_kernel(tc, x, weights, bias, center, sig
             for s in range(pieces):
                 nc.sync.dma_start(out=x_sb[c][:, s * width:(s + 1) * width], in_=xv[:, c, s * width:(s + 1) * width])
 
-        nc.sync.dma_start(out=w_sb[:].rearrange("p (h k) -> p h k", h=2),
-                          in_=weights.rearrange("(h p) k -> p h k", h=2))
+        for h in range(2):
+            nc.sync.dma_start(out=w_sb[:, h * K:(h + 1) * K], in_=weights[h * P:(h + 1) * P, :])
         load_x(0, 2)
         nc.sync.dma_start(out=vec[0:1, 0:N], in_=bias.unsqueeze(0))
         nc.sync.dma_start(out=vec[0:1, N:2 * N], in_=sigma.unsqueeze(0))
@@ -254,22 +254,24 @@ def tile_orthogonallyattenuatedlinear_t_kernel(tc, x, weights, bias, center, sig
             nc.vector.tensor_copy(out=zs[:], in_=st[("zt", j)][:])
             st[("zs", j)] = zs
 
-        def t2_op(j, bank=None):
+        def t2_mm(j, b, bank=None):
             if not ok(j):
                 return
-            tbs = []
-            for b in range(2):
-                pool, tag = bank or (ps_t, "tb")
-                tp = pool.tile([P, 2, N], F32, name="tb", tag=tag)
-                nc.tensor.matmul(tp[:], lhsT=st[("zs", j)][:], rhs=rk[:, 2 * b:2 * b + 2, :], start=True, stop=False)
-                tbs.append(tp)
+            pool, tag = bank or (ps_t, "tb")
+            tp = pool.tile([P, 2, N], F32, name="tb", tag=tag)
+            nc.tensor.matmul(tp[:], lhsT=st[("zs", j)][:], rhs=rk[:, 2 * b:2 * b + 2, :], start=True, stop=False)
+            st[("tb", j, b)] = tp
+
+        def t2_tr(j):
+            if not ok(j):
+                return
             for b in range(2):
                 for tt in range(2):
                     for h in range(2):
                         t = 2 * b + tt
-                        nc.tensor.matmul(tbs[b][:, tt, h * P:(h + 1) * P], lhsT=st[("u", j, h)][:, t * P:(t + 1) * P],
-                                         rhs=ident_f[:], is_transpose=True, start=False, stop=tt == 1 and h == 1)
-                st[("tb", j, b)] = tbs[b]
+                        nc.tensor.matmul(st[("tb", j, b)][:, tt, h * P:(h + 1) * P],
+                                         lhsT=st[("u", j, h)][:, t * P:(t + 1) * P], rhs=ident_f[:],
+                                         is_transpose=True, start=False, stop=tt == 1 and h == 1)
 
         def ex(j, t0, nt):
             if not ok(j):
@@ -297,22 +299,22 @@ def tile_orthogonallyattenuatedlinear_t_kernel(tc, x, weights, bias, center, sig
         nc.scalar.activation(out=junk_w[:], in_=w_half(w_sb, 1), func=ACT.Square, accum_out=ss[:, 1:2])
         nc.gpsimd.tensor_scalar_max(out=ss[:], in0=ss[:], scalar1=1e-24)
         nc.gpsimd.tensor_tensor(out=rinv[:], in0=ss[:], in1=mhalf[:], op=ALU.pow)
+        w_tp = words_transposed(w_sb, "w")
         t1(0)
         sg_ps = ps_a.tile([P, 2, P], BF16, name="sg_ps", tag="a")
         for h in range(2):
             nc.tensor.transpose(sg_ps[:, h, :], vec[:, N + h * P:N + (h + 1) * P], ident_b[:])
         c_tp = words_transposed(c_sb, "c")
-        w_tp = words_transposed(w_sb, "w")
         for h in range(2):
             nc.scalar.activation(out=junk_w[:], in_=w_half(c_sb, h), func=ACT.Square, accum_out=c2[:, h:h + 1])
         x2_rows(0, [0, 1])
         words_out(c_tp, c_grp, nc.scalar.copy)
         x2_rows(0, [2, 3])
+        words_out(w_tp, w_grp, nc.vector.tensor_copy)
         ev(0)
         nc.vector.reciprocal(out=rs[:], in_=sg_ps[:, :, 0])
         nc.vector.scalar_tensor_tensor(out=coef[:, 0, :], in0=rs[:], scalar=-1.0, in1=rs[:],
                                        op0=ALU.mult, op1=ALU.mult)
-        words_out(w_tp, w_grp, nc.vector.tensor_copy)
         for h in range(2):
             nc.vector.tensor_scalar(out=w_half(wn, h), in0=w_half(w_sb, h), scalar1=rinv[:, h:h + 1], scalar2=None,
                                     op0=ALU.mult)
@@ -328,15 +330,16 @@ def tile_orthogonallyattenuatedlinear_t_kernel(tc, x, weights, bias, center, sig
             for t in range(4):
                 nc.tensor.matmul(cw_ps[:, h, :], lhsT=c4[:, h * P:(h + 1) * P, t], rhs=w4[:, h * P:(h + 1) * P, t],
                                  start=t == 0, stop=t == 3)
-        words_out(wn_tp, wn_grp, nc.vector.tensor_copy)
+
         quant(0)
+        words_out(wn_tp, wn_grp, nc.vector.tensor_copy)
+        nc.vector.quantize_mx(out=c_codes[:].bitcast(FP8X4), scales=c_scales[:], in_=c_grp[:])
+        nc.vector.quantize_mx(out=wn_codes[:].bitcast(FP8X4), scales=wn_scales[:], in_=wn_grp[:])
         for h in range(2):
             nc.vector.scalar_tensor_tensor(out=junk_c[:], in0=cw_ps[:, h, :], scalar=rinv[:, h:h + 1], in1=ident_f[:],
                                            op0=ALU.mult, op1=ALU.mult, accum_out=cw[:, h:h + 1])
-        nc.vector.quantize_mx(out=wn_codes[:].bitcast(FP8X4), scales=wn_scales[:], in_=wn_grp[:])
         nc.vector.scalar_tensor_tensor(out=is2x2[:], in0=rs[:], scalar=2.0, in1=rs[:], op0=ALU.mult, op1=ALU.mult)
         nc.vector.scalar_tensor_tensor(out=nb[:], in0=cw[:], scalar=-1.0, in1=rs[:], op0=ALU.mult, op1=ALU.mult)
-        nc.vector.quantize_mx(out=c_codes[:].bitcast(FP8X4), scales=c_scales[:], in_=c_grp[:])
         nc.vector.quantize_mx(out=w_codes[:].bitcast(FP8X4), scales=w_scales[:], in_=w_grp[:])
 
         nc.gpsimd.tensor_tensor(out=coef[:, 1, :], in0=coef[:, 0, :], in1=c2[:], op=ALU.mult)
@@ -370,11 +373,13 @@ def tile_orthogonallyattenuatedlinear_t_kernel(tc, x, weights, bias, center, sig
             sq(j + 1, 1)
             pw_op(j, 0)
             m_a(j, 1)
+            t2_mm(j, 0)
+            t2_mm(j, 1)
             ev(j + 2, [1])
             u_op(j, 1)
             t1(j + 3)
             z_t(j + 1)
-            t2_op(j)
+            t2_tr(j)
             x2_rows(j + 2, [1, 2] if j in (0, 4) else [1, 2, 3])
             pw_op(j, 1)
             ex(j, 0, 2)
@@ -403,7 +408,9 @@ def tile_orthogonallyattenuatedlinear_t_kernel(tc, x, weights, bias, center, sig
         u_op(i, 1)
         m_bc(j, 1, "c", spare)
         z_t(j)
-        t2_op(i)
+        t2_mm(i, 0)
+        t2_mm(i, 1)
+        t2_tr(i)
         ex(i, 0, 2)
         ex(i, 2, 2)
         u_op(j, 0)
@@ -412,7 +419,9 @@ def tile_orthogonallyattenuatedlinear_t_kernel(tc, x, weights, bias, center, sig
         mul(i, 0, 2, nc.gpsimd)
         u_op(j, 1)
         m_a(j, 1, spare)
-        t2_op(j, (ps_b, "b"))
+        t2_mm(j, 0, (ps_b, "b"))
+        t2_mm(j, 1, (ps_b, "b"))
+        t2_tr(j)
         pw_op(j, 0)
         pw_op(j, 1)
         mul(i, 2, 2, nc.vector)

@@ -296,7 +296,8 @@ def tile_orthogonallyattenuatedlinear_t_kernel(tc, x, weights, bias, center, sig
             return t[:, h * K:(h + 1) * K]
 
         nc.scalar.activation(out=junk_w[:], in_=w_half(w_sb, 0), func=ACT.Square, accum_out=ss[:, 0:1])
-        nc.scalar.activation(out=junk_w[:], in_=w_half(w_sb, 1), func=ACT.Square, accum_out=ss[:, 1:2])
+        nc.vector.scalar_tensor_tensor(out=junk_v[:], in0=w_half(w_sb, 1), scalar=1.0, in1=w_half(w_sb, 1),
+                                       op0=ALU.mult, op1=ALU.mult, accum_out=ss[:, 1:2])
         nc.gpsimd.tensor_scalar_max(out=ss[:], in0=ss[:], scalar1=1e-24)
         nc.gpsimd.tensor_tensor(out=rinv[:], in0=ss[:], in1=mhalf[:], op=ALU.pow)
         w_tp = words_transposed(w_sb, "w")
@@ -305,9 +306,10 @@ def tile_orthogonallyattenuatedlinear_t_kernel(tc, x, weights, bias, center, sig
         for h in range(2):
             nc.tensor.transpose(sg_ps[:, h, :], vec[:, N + h * P:N + (h + 1) * P], ident_b[:])
         c_tp = words_transposed(c_sb, "c")
+        x2_rows(0, [0])
         for h in range(2):
             nc.scalar.activation(out=junk_w[:], in_=w_half(c_sb, h), func=ACT.Square, accum_out=c2[:, h:h + 1])
-        x2_rows(0, [0, 1])
+        x2_rows(0, [1])
         words_out(c_tp, c_grp, nc.scalar.copy)
         x2_rows(0, [2, 3])
         words_out(w_tp, w_grp, nc.vector.tensor_copy)
@@ -356,31 +358,32 @@ def tile_orthogonallyattenuatedlinear_t_kernel(tc, x, weights, bias, center, sig
                                   in_=piece[:, 1, :].unsqueeze(2).to_broadcast([P, 2, TPC]))
         z_split(0)
         x2_rows(1, [0, 1])
+        m_bc(0, 0, "b")
+        m_bc(0, 1, "b")
         rk_ps = ps_t.tile([P, TPC, N], BF16, name="rk_ps", tag="tb")
         for t in range(TPC):
             for h in range(2):
                 nc.tensor.transpose(rk_ps[:, t, h * P:(h + 1) * P], zr[:, h, t * P:(t + 1) * P], ident_b[:])
-        nc.scalar.copy(out=rk[:], in_=rk_ps[:])
-        m_bc(0, 0, "b")
-        m_bc(0, 1, "b")
 
         for j in range(-1, NCH - 2):
             ev(j + 2, [0])
             u_op(j, 0)
+            t2_mm(j, 0)
             m_bc(j, 1, "c")
-            x2_rows(j + 2, [0])
+            x2_rows(j + 2, [] if j == -1 else [0])
             sq(j + 1, 0)
             sq(j + 1, 1)
+            if j == -1:
+                nc.scalar.copy(out=rk[:], in_=rk_ps[:])
             pw_op(j, 0)
-            m_a(j, 1)
-            t2_mm(j, 0)
             t2_mm(j, 1)
+            m_a(j, 1)
             ev(j + 2, [1])
             u_op(j, 1)
             t1(j + 3)
             z_t(j + 1)
             t2_tr(j)
-            x2_rows(j + 2, [1, 2] if j in (0, 4) else [1, 2, 3])
+            x2_rows(j + 2, [0, 1, 2, 3] if j == -1 else [1, 2] if j in (0, 4) else [1, 2, 3])
             pw_op(j, 1)
             ex(j, 0, 2)
             ex(j, 2, 2)

@@ -177,7 +177,7 @@ def tile_orthogonallyattenuatedlinear_t_kernel(tc, x, weights, bias, center, sig
             st[("q", j)] = (codes, scales)
 
         def m_a(j, b, bank=None):
-            if not ok(j):
+            if not ok(j) or ("a", j, b) in st:
                 return
             codes, scales = st[("q", j)]
             pool, tag = bank or (ps_a, "a")
@@ -323,18 +323,19 @@ def tile_orthogonallyattenuatedlinear_t_kernel(tc, x, weights, bias, center, sig
         wn_tp = words_transposed(wn, "wn", ps_b, "b")
         bs_ps = ps_b.tile([P, N], F32, name="bs_ps", tag="b")
         nc.tensor.matmul(bs_ps[:], lhsT=ones_b[:], rhs=vec[:, 0:N], start=True, stop=True)
-        t1(1)
         nc.scalar.copy(out=bias_sb[:], in_=bs_ps[:])
-        cw_ps = ps_c.tile([P, 2, P], F32, name="cw_ps", tag="c")
+        quant(0)
+        nc.vector.quantize_mx(out=w_codes[:].bitcast(FP8X4), scales=w_scales[:], in_=w_grp[:])
+        cw_ps = ps_t.tile([P, 2, P], F32, name="cw_ps", tag="tb")
         c4 = c_grp[:].rearrange("p (c t) -> p c t", t=4)
         w4 = w_grp[:].rearrange("p (c t) -> p c t", t=4)
         for h in range(2):
             for t in range(4):
                 nc.tensor.matmul(cw_ps[:, h, :], lhsT=c4[:, h * P:(h + 1) * P, t], rhs=w4[:, h * P:(h + 1) * P, t],
                                  start=t == 0, stop=t == 3)
-
-        quant(0)
         words_out(wn_tp, wn_grp, nc.vector.tensor_copy)
+        m_a(0, 0)
+        t1(1)
         nc.vector.quantize_mx(out=c_codes[:].bitcast(FP8X4), scales=c_scales[:], in_=c_grp[:])
         nc.vector.quantize_mx(out=wn_codes[:].bitcast(FP8X4), scales=wn_scales[:], in_=wn_grp[:])
         for h in range(2):
@@ -342,7 +343,9 @@ def tile_orthogonallyattenuatedlinear_t_kernel(tc, x, weights, bias, center, sig
                                            op0=ALU.mult, op1=ALU.mult, accum_out=cw[:, h:h + 1])
         nc.vector.scalar_tensor_tensor(out=is2x2[:], in0=rs[:], scalar=2.0, in1=rs[:], op0=ALU.mult, op1=ALU.mult)
         nc.vector.scalar_tensor_tensor(out=nb[:], in0=cw[:], scalar=-1.0, in1=rs[:], op0=ALU.mult, op1=ALU.mult)
-        nc.vector.quantize_mx(out=w_codes[:].bitcast(FP8X4), scales=w_scales[:], in_=w_grp[:])
+        m_bc(0, 0, "b")
+        m_bc(0, 1, "b")
+        m_bc(0, 0, "c")
 
         nc.gpsimd.tensor_tensor(out=coef[:, 1, :], in0=coef[:, 0, :], in1=c2[:], op=ALU.mult)
         nc.gpsimd.tensor_copy(out=ph[:], in_=coef[:])
@@ -358,8 +361,6 @@ def tile_orthogonallyattenuatedlinear_t_kernel(tc, x, weights, bias, center, sig
                                   in_=piece[:, 1, :].unsqueeze(2).to_broadcast([P, 2, TPC]))
         z_split(0)
         x2_rows(1, [0, 1])
-        m_bc(0, 0, "b")
-        m_bc(0, 1, "b")
         rk_ps = ps_t.tile([P, TPC, N], BF16, name="rk_ps", tag="tb")
         for t in range(TPC):
             for h in range(2):
@@ -402,6 +403,8 @@ def tile_orthogonallyattenuatedlinear_t_kernel(tc, x, weights, bias, center, sig
         spare = (ps_x, "xt")
         m_bc(i, 1, "c", spare)
         m_a(i, 1, spare)
+        t2_mm(i, 0)
+        t2_mm(i, 1)
         sq(j, 0)
         sq(j, 1)
         u_op(i, 0)
@@ -409,21 +412,19 @@ def tile_orthogonallyattenuatedlinear_t_kernel(tc, x, weights, bias, center, sig
         pw_op(i, 0)
         m_a(j, 0)
         u_op(i, 1)
-        m_bc(j, 1, "c", spare)
         z_t(j)
-        t2_mm(i, 0)
-        t2_mm(i, 1)
         t2_tr(i)
+        m_bc(j, 1, "c", spare)
         ex(i, 0, 2)
         ex(i, 2, 2)
         u_op(j, 0)
         z_out(j)
         pw_op(i, 1)
         mul(i, 0, 2, nc.gpsimd)
-        u_op(j, 1)
         m_a(j, 1, spare)
         t2_mm(j, 0, (ps_b, "b"))
         t2_mm(j, 1, (ps_b, "b"))
+        u_op(j, 1)
         t2_tr(j)
         pw_op(j, 0)
         pw_op(j, 1)

@@ -384,11 +384,11 @@ def tile_orthogonallyattenuatedlinear_t_kernel(tc, x, weights, bias, center, sig
             t1(j + 3)
             z_t(j + 1)
             t2_tr(j)
-            x2_rows(j + 2, [0, 1, 2, 3] if j == -1 else [1, 2] if j in (0, 4) else [1, 2, 3])
+            x2_rows(j + 2, [0, 1, 2] if j == -1 else [1, 2] if j in (1, 3,) else [1, 2, 3])
             pw_op(j, 1)
             ex(j, 0, 2)
             ex(j, 2, 2)
-            if j in (0, 4):
+            if j in (-1, 1, 3):
                 x2_vec(j + 2, 3)
             m_bc(j + 1, 0, "c")
             m_a(j + 1, 0)

@@ -72,9 +72,9 @@ def tile_orthogonallyattenuatedlinear_t_kernel(tc, x, weights, bias, center, sig
         x2 = const.tile([P, NCH * TPC], F32, name="x2")
 
         def quantised(name, width):
-            codes = const.tile([P, width], U32, name=name + "_codes", align_bytes=64)
-            scales = const.tile([P, width], U8, name=name + "_scales", align_bytes=64)
-            return codes, scales
+            codes = const.tile([P, 32 + width], U32, name=name + "_codes", align_bytes=256)
+            scales = const.tile([P, 192 + width], U8, name=name + "_scales", align_bytes=256)
+            return codes[:, 32:32 + width], scales[:, 192:192 + width]
 
         junk_w = const.tile([P, K], BF16, name="junk_w")
         junk_c = const.tile([P, P], F32, name="junk_c")
@@ -171,8 +171,9 @@ def tile_orthogonallyattenuatedlinear_t_kernel(tc, x, weights, bias, center, sig
         def quant(j):
             if not ok(j):
                 return
-            codes = work.tile([P, CW], U32, name="xcodes", tag="xcodes", bufs=4, align_bytes=64)
-            scales = work.tile([P, CW], U8, name="xscales", tag="xscales", bufs=4, align_bytes=64)
+            codes = work.tile([P, CW], U32, name="xcodes", tag="xcodes", bufs=4, align_bytes=256)
+            scales_tile = work.tile([P, 64 + CW], U8, name="xscales", tag="xscales", bufs=4, align_bytes=256)
+            scales = scales_tile[:, 64:64 + CW]
             nc.vector.quantize_mx(out=codes[:].bitcast(FP8X4), scales=scales[:], in_=st[("grp", j)][:])
             st[("q", j)] = (codes, scales)
 

@@ -38,10 +38,11 @@ def tile_orthogonallyattenuatedlinear_t_kernel(tc, x, weights, bias, center, sig
 
         w_sb = const.tile([P, 2 * K], BF16, name="w_sb")
         c_sb = const.tile([P, 2 * K], BF16, name="c_sb")
-        vec = const.tile([P, 2 * N], BF16, name="vec")
+        sig = const.tile([P, N], BF16, name="sig")
+        bias_sb = const.tile([P, N], BF16, name="bias_sb")
         one1 = const.tile([P, 1], F32, name="one1")
         nc.vector.memset(one1[:], 1.0)
-        nc.vector.memset(vec[:], 0.0)
+        nc.vector.memset(sig[:], 0.0)
         x_sb = [xpool.tile([P, TPC * K], BF16, name="x%d" % c) for c in range(NCH)]
 
         def load_x(c, pieces):
@@ -52,11 +53,12 @@ def tile_orthogonallyattenuatedlinear_t_kernel(tc, x, weights, bias, center, sig
         for h in range(2):
             nc.sync.dma_start(out=w_sb[:, h * K:(h + 1) * K], in_=weights[h * P:(h + 1) * P, :])
         load_x(0, 2)
-        nc.sync.dma_start(out=vec[0:1, 0:N], in_=bias.unsqueeze(0))
-        nc.sync.dma_start(out=vec[0:1, N:2 * N], in_=sigma.unsqueeze(0))
+        nc.sync.dma_start(out=sig[0:1, :], in_=sigma.unsqueeze(0))
         nc.sync.dma_start(out=c_sb[:].rearrange("p (h k) -> p h k", h=2),
                           in_=center.rearrange("(h p) k -> p h k", h=2))
         for c in range(1, NCH):
+            if c == 4:
+                nc.sync.dma_start(out=bias_sb[:], in_=bias.partition_broadcast(P))
             load_x(c, 1)
 
         dummy = const.tile([P, 1], F32, name="dummy")
@@ -67,8 +69,6 @@ def tile_orthogonallyattenuatedlinear_t_kernel(tc, x, weights, bias, center, sig
         masks.make_identity(nc, ident_f[:])
         ident_b = const.tile([P, P], BF16, name="ident_b")
         nc.vector.tensor_copy(out=ident_b[:], in_=ident_f[:])
-        ones_b = const.tile([P, P], BF16, name="ones_b")
-        nc.vector.memset(ones_b[:], 1.0)
         x2 = const.tile([P, NCH * TPC], F32, name="x2")
 
         def quantised(name, width):
@@ -91,15 +91,20 @@ def tile_orthogonallyattenuatedlinear_t_kernel(tc, x, weights, bias, center, sig
         c_grp = const.tile([P, 4 * N], BF16, name="c_grp", align_bytes=64)
         wn_grp = const.tile([P, 4 * N], BF16, name="wn_grp", align_bytes=64)
         wn = const.tile([P, 2 * K], BF16, name="wn")
-        bias_sb = const.tile([P, N], F32, name="bias_sb")
         rs = const.tile([P, 2], F32, name="rs")
         is2x2 = const.tile([P, 2], F32, name="is2x2")
         coef = const.tile([P, 2, 2], F32, name="coef")
         res = const.tile([P, 2, 2], F32, name="res")
-        ph = const.tile([P, 2, 2], BF16, name="ph")
-        pm = const.tile([P, 2, 2], BF16, name="pm")
-        pl = const.tile([P, 2, 2], BF16, name="pl")
-        zr = const.tile([P, 2, TPC * P], BF16, name="zr")
+        pc = const.tile([P, 2, 2, 3], BF16, name="pc")
+        zr = const.tile([P, 2, P], BF16, name="zr")
+        zrt = const.tile([P, N], BF16, name="zrt")
+        mask = const.tile([P, TPC], F32, name="mask")
+        mask_c = const.tile([P, 1], F32, name="mask_c")
+        nc.vector.tensor_reduce(out=mask[:], in_=ident_f[:, 0:NK * TPC].rearrange("p (k t) -> p t k", t=TPC),
+                                op=ALU.add, axis=mybir.AxisListType.X)
+        nc.vector.tensor_reduce(out=mask_c[:], in_=ident_f[:, NK * TPC:NK * TPC + 3],
+                                op=ALU.add, axis=mybir.AxisListType.X)
+        nc.vector.tensor_scalar(out=mask[:], in0=mask[:], scalar1=mask_c[:], scalar2=None, op0=ALU.add)
         rk = const.tile([P, TPC, N], BF16, name="rk")
         nc.vector.memset(zr[:], 0.0)
         z = []
@@ -302,31 +307,30 @@ def tile_orthogonallyattenuatedlinear_t_kernel(tc, x, weights, bias, center, sig
         nc.gpsimd.tensor_scalar_max(out=ss[:], in0=ss[:], scalar1=1e-24)
         nc.gpsimd.tensor_tensor(out=rinv[:], in0=ss[:], in1=mhalf[:], op=ALU.pow)
         w_tp = words_transposed(w_sb, "w")
+        words_out(w_tp, w_grp, nc.vector.tensor_copy)
         t1(0)
         sg_ps = ps_a.tile([P, 2, P], BF16, name="sg_ps", tag="a")
         for h in range(2):
-            nc.tensor.transpose(sg_ps[:, h, :], vec[:, N + h * P:N + (h + 1) * P], ident_b[:])
+            nc.tensor.transpose(sg_ps[:, h, :], sig[:, h * P:(h + 1) * P], ident_b[:])
         c_tp = words_transposed(c_sb, "c")
-        x2_rows(0, [0])
-        for h in range(2):
-            nc.scalar.activation(out=junk_w[:], in_=w_half(c_sb, h), func=ACT.Square, accum_out=c2[:, h:h + 1])
-        x2_rows(0, [1])
+        x2_rows(0, [0, 1])
+        nc.scalar.activation(out=junk_w[:], in_=w_half(c_sb, 0), func=ACT.Square, accum_out=c2[:, 0:1])
+        nc.scalar.activation(out=junk_w[:], in_=w_half(c_sb, 1), func=ACT.Square, accum_out=c2[:, 1:2])
         words_out(c_tp, c_grp, nc.scalar.copy)
         x2_rows(0, [2, 3])
-        words_out(w_tp, w_grp, nc.vector.tensor_copy)
-        ev(0)
-        nc.vector.reciprocal(out=rs[:], in_=sg_ps[:, :, 0])
-        nc.vector.scalar_tensor_tensor(out=coef[:, 0, :], in0=rs[:], scalar=-1.0, in1=rs[:],
-                                       op0=ALU.mult, op1=ALU.mult)
+        ev(0, [0])
         for h in range(2):
             nc.vector.tensor_scalar(out=w_half(wn, h), in0=w_half(w_sb, h), scalar1=rinv[:, h:h + 1], scalar2=None,
                                     op0=ALU.mult)
         wn_tp = words_transposed(wn, "wn", ps_b, "b")
-        bs_ps = ps_b.tile([P, N], F32, name="bs_ps", tag="b")
-        nc.tensor.matmul(bs_ps[:], lhsT=ones_b[:], rhs=vec[:, 0:N], start=True, stop=True)
-        nc.scalar.copy(out=bias_sb[:], in_=bs_ps[:])
-        quant(0)
+        ev(0, [1])
         nc.vector.quantize_mx(out=w_codes[:].bitcast(FP8X4), scales=w_scales[:], in_=w_grp[:])
+        nc.vector.reciprocal(out=rs[:], in_=sg_ps[:, :, 0])
+        quant(0)
+        nc.vector.scalar_tensor_tensor(out=coef[:, 0, :], in0=rs[:], scalar=-1.0, in1=rs[:],
+                                       op0=ALU.mult, op1=ALU.mult)
+        words_out(wn_tp, wn_grp, nc.vector.tensor_copy)
+        t1(1)
         cw_ps = ps_t.tile([P, 2, P], F32, name="cw_ps", tag="tb")
         c4 = c_grp[:].rearrange("p (c t) -> p c t", t=4)
         w4 = w_grp[:].rearrange("p (c t) -> p c t", t=4)
@@ -334,49 +338,57 @@ def tile_orthogonallyattenuatedlinear_t_kernel(tc, x, weights, bias, center, sig
             for t in range(4):
                 nc.tensor.matmul(cw_ps[:, h, :], lhsT=c4[:, h * P:(h + 1) * P, t], rhs=w4[:, h * P:(h + 1) * P, t],
                                  start=t == 0, stop=t == 3)
-        words_out(wn_tp, wn_grp, nc.vector.tensor_copy)
         m_a(0, 0)
-        t1(1)
-        nc.vector.quantize_mx(out=c_codes[:].bitcast(FP8X4), scales=c_scales[:], in_=c_grp[:])
         nc.vector.quantize_mx(out=wn_codes[:].bitcast(FP8X4), scales=wn_scales[:], in_=wn_grp[:])
         for h in range(2):
             nc.vector.scalar_tensor_tensor(out=junk_c[:], in0=cw_ps[:, h, :], scalar=rinv[:, h:h + 1], in1=ident_f[:],
                                            op0=ALU.mult, op1=ALU.mult, accum_out=cw[:, h:h + 1])
         nc.vector.scalar_tensor_tensor(out=is2x2[:], in0=rs[:], scalar=2.0, in1=rs[:], op0=ALU.mult, op1=ALU.mult)
         nc.vector.scalar_tensor_tensor(out=nb[:], in0=cw[:], scalar=-1.0, in1=rs[:], op0=ALU.mult, op1=ALU.mult)
+        nc.vector.quantize_mx(out=c_codes[:].bitcast(FP8X4), scales=c_scales[:], in_=c_grp[:])
         m_bc(0, 0, "b")
         m_bc(0, 1, "b")
         m_bc(0, 0, "c")
-
         nc.gpsimd.tensor_tensor(out=coef[:, 1, :], in0=coef[:, 0, :], in1=c2[:], op=ALU.mult)
-        nc.gpsimd.tensor_copy(out=ph[:], in_=coef[:])
-        nc.gpsimd.tensor_tensor(out=res[:], in0=coef[:], in1=ph[:], op=ALU.subtract)
-        nc.gpsimd.tensor_copy(out=pm[:], in_=res[:])
-        nc.gpsimd.tensor_tensor(out=pl[:], in0=res[:], in1=pm[:], op=ALU.subtract)
-        for k, piece in enumerate([ph, pm, pl, ph, pm, ph]):
-            nc.gpsimd.tensor_copy(out=zr[:, :, k * TPC:k * TPC + (TPC - 1) * (P + 1) + 1:P + 1],
-                                  in_=piece[:, 0, :].unsqueeze(2).to_broadcast([P, 2, TPC]))
-        for k, piece in enumerate([ph, pm, pl]):
-            c0 = NK * TPC + k
-            nc.gpsimd.tensor_copy(out=zr[:, :, c0:c0 + (TPC - 1) * P + 1:P],
-                                  in_=piece[:, 1, :].unsqueeze(2).to_broadcast([P, 2, TPC]))
+        nc.gpsimd.tensor_copy(out=pc[:, :, :, 0], in_=coef[:])
+        nc.gpsimd.tensor_tensor(out=res[:], in0=coef[:], in1=pc[:, :, :, 0], op=ALU.subtract)
+        nc.gpsimd.tensor_copy(out=pc[:, :, :, 1], in_=res[:])
+        nc.gpsimd.tensor_tensor(out=pc[:, :, :, 2], in0=res[:], in1=pc[:, :, :, 1], op=ALU.subtract)
+        for k0, count in [(0, 3), (3, 2), (5, 1)]:
+            nc.gpsimd.tensor_copy(
+                out=zr[:, :, k0 * TPC:(k0 + count) * TPC].rearrange("p h (k t) -> p h k t", t=TPC),
+                in_=pc[:, 0, :, 0:count].unsqueeze(3).to_broadcast([P, 2, count, TPC]))
+        nc.gpsimd.tensor_copy(out=zr[:, :, NK * TPC:NK * TPC + 3], in_=pc[:, 1, :, :])
         z_split(0)
-        x2_rows(1, [0, 1])
-        rk_ps = ps_t.tile([P, TPC, N], BF16, name="rk_ps", tag="tb")
+        x2_rows(1, [0, 1, 2])
+        sq(0, 0)
+        sq(0, 1)
+        rk_ps = ps_t.tile([P, N], BF16, name="rk_ps", tag="tb")
+        for h in range(2):
+            nc.tensor.transpose(rk_ps[:, h * P:(h + 1) * P], zr[:, h, :], ident_b[:])
+        nc.scalar.copy(out=zrt[:], in_=rk_ps[:])
         for t in range(TPC):
-            for h in range(2):
-                nc.tensor.transpose(rk_ps[:, t, h * P:(h + 1) * P], zr[:, h, t * P:(t + 1) * P], ident_b[:])
+            nc.gpsimd.tensor_scalar(out=rk[:, t, :], in0=zrt[:], scalar1=mask[:, t:t + 1], scalar2=0.0,
+                                    op0=ALU.mult, op1=ALU.add)
+        ev(1, [0])
+        ev(1, [1])
+        t1(2)
+        z_t(0)
+        x2_rows(1, [3])
+        quant(1)
+        z_out(0)
+        m_bc(1, 0, "b")
+        m_bc(1, 1, "b")
+        z_split(1)
 
-        for j in range(-1, NCH - 2):
+        for j in range(NCH - 2):
             ev(j + 2, [0])
             u_op(j, 0)
             t2_mm(j, 0)
             m_bc(j, 1, "c")
-            x2_rows(j + 2, [] if j == -1 else [0])
+            x2_rows(j + 2, [0])
             sq(j + 1, 0)
             sq(j + 1, 1)
-            if j == -1:
-                nc.scalar.copy(out=rk[:], in_=rk_ps[:])
             pw_op(j, 0)
             t2_mm(j, 1)
             m_a(j, 1)
@@ -385,11 +397,11 @@ def tile_orthogonallyattenuatedlinear_t_kernel(tc, x, weights, bias, center, sig
             t1(j + 3)
             z_t(j + 1)
             t2_tr(j)
-            x2_rows(j + 2, [0, 1, 2] if j == -1 else [1, 2] if j in (1, 3,) else [1, 2, 3])
+            x2_rows(j + 2, [1, 2] if j in (1, 3,) else [1, 2, 3])
             pw_op(j, 1)
             ex(j, 0, 2)
             ex(j, 2, 2)
-            if j in (-1, 1, 3):
+            if j in (1, 3):
                 x2_vec(j + 2, 3)
             m_bc(j + 1, 0, "c")
             m_a(j + 1, 0)

@@ -381,7 +381,7 @@ def tile_orthogonallyattenuatedlinear_t_kernel(tc, x, weights, bias, center, sig
         m_bc(1, 1, "b")
         z_split(1)
 
-        for j in range(NCH - 2):
+        for j in range(NCH - 3):
             ev(j + 2, [0])
             u_op(j, 0)
             t2_mm(j, 0)
@@ -412,35 +412,61 @@ def tile_orthogonallyattenuatedlinear_t_kernel(tc, x, weights, bias, center, sig
             z_split(j + 2)
             mul(j, 0, TPC, nc.gpsimd)
 
-        i, j = NCH - 2, NCH - 1
+        g, i, j = NCH - 3, NCH - 2, NCH - 1
         spare = (ps_x, "xt")
+        ev(j, [0])
+        u_op(g, 0)
+        t2_mm(g, 0)
+        m_bc(g, 1, "c")
+        x2_rows(j, [0])
+        sq(i, 0)
+        sq(i, 1)
+        pw_op(g, 0)
+        t2_mm(g, 1)
+        m_a(g, 1)
+        ev(j, [1])
+        u_op(g, 1)
         m_bc(i, 1, "c", spare)
+        z_t(i)
+        t2_tr(g)
+        x2_rows(j, [1, 2, 3])
+        pw_op(g, 1)
+        ex(g, 0, 2)
+        ex(g, 2, 2)
+        quant(j)
+        z_out(i)
+        m_bc(i, 0, "c")
+        m_a(i, 0)
         m_a(i, 1, spare)
-        t2_mm(i, 0)
-        t2_mm(i, 1)
+        m_bc(j, 0, "b")
+        m_bc(j, 1, "b")
+        z_split(j)
+        mul(g, 0, TPC, nc.gpsimd)
         sq(j, 0)
         sq(j, 1)
         u_op(i, 0)
+        u_op(i, 1)
+        t2_mm(i, 0)
         m_bc(j, 0, "c")
         pw_op(i, 0)
-        m_a(j, 0)
-        u_op(i, 1)
+        pw_op(i, 1)
+        t2_mm(i, 1)
+        m_bc(j, 1, "c", spare)
         z_t(j)
         t2_tr(i)
-        m_bc(j, 1, "c", spare)
         ex(i, 0, 2)
         ex(i, 2, 2)
         u_op(j, 0)
         z_out(j)
-        pw_op(i, 1)
-        mul(i, 0, 2, nc.gpsimd)
+        u_op(j, 1)
+        m_a(j, 0)
         m_a(j, 1, spare)
         t2_mm(j, 0, (ps_b, "b"))
         t2_mm(j, 1, (ps_b, "b"))
-        u_op(j, 1)
         t2_tr(j)
         pw_op(j, 0)
         pw_op(j, 1)
+        mul(i, 0, 2, nc.gpsimd)
         mul(i, 2, 2, nc.vector)
         for t in range(TPC):
             ex(j, t, 1)

@@ -107,12 +107,9 @@ def tile_orthogonallyattenuatedlinear_t_kernel(tc, x, weights, bias, center, sig
         nc.vector.tensor_scalar(out=mask[:], in0=mask[:], scalar1=mask_c[:], scalar2=None, op0=ALU.add)
         rk = const.tile([P, TPC, N], BF16, name="rk")
         nc.vector.memset(zr[:], 0.0)
-        z = []
-        for i in range(3):
-            z_i = const.tile([P, P], BF16, name="z%d" % i)
-            nc.gpsimd.memset(z_i[:], 0.0)
-            nc.gpsimd.memset(z_i[:, NK * TPC:NK * TPC + 3], 1.0)
-            z.append(z_i)
+        z = const.tile([P, 3, P], BF16, name="z")
+        nc.vector.memset(z[:], 0.0)
+        nc.vector.memset(z[:, :, NK * TPC:NK * TPC + 3], 1.0)
         bias_b = bias_sb[:].unsqueeze(1).to_broadcast([P, 2, N])
 
         def words_transposed(src, name, pool=ps_t, tag="tb"):
@@ -137,19 +134,9 @@ def tile_orthogonallyattenuatedlinear_t_kernel(tc, x, weights, bias, center, sig
             if not ok(j):
                 return
             for t in tiles:
-                if ("x2", j, t) in st:
-                    continue
-                st[("x2", j, t)] = True
                 junk = work.tile([P, K], BF16, name="junk", tag="junk")
                 nc.scalar.activation(out=junk[:], in_=x_sb[j][:, t * K:(t + 1) * K], func=ACT.Square,
                                      accum_out=x2[:, j * TPC + t:j * TPC + t + 1])
-
-        def x2_vec(j, t):
-            if not ok(j):
-                return
-            xt = x_sb[j][:, t * K:(t + 1) * K]
-            nc.vector.scalar_tensor_tensor(out=junk_v[:], in0=xt, scalar=1.0, in1=xt, op0=ALU.mult, op1=ALU.mult,
-                                           accum_out=x2[:, j * TPC + t:j * TPC + t + 1])
 
         def t1(j, halves=(0, 1)):
             if not ok(j):
@@ -233,12 +220,9 @@ def tile_orthogonallyattenuatedlinear_t_kernel(tc, x, weights, bias, center, sig
                                     in1=bias_b, op=ALU.add)
 
         def z_split(j):
-            if ("z", j) in st:
-                return
-            st[("z", j)] = True
             if not ok(j):
                 return
-            zt = z[j % 3][:].rearrange("p (k t) -> p k t", t=TPC)
+            zt = z[:, j % 3, :].rearrange("p (k t) -> p k t", t=TPC)
             xc = x2[:, j * TPC:(j + 1) * TPC]
             r1 = work.tile([P, TPC], F32, name="r1", tag="r1")
             nc.gpsimd.tensor_copy(out=zt[:, 0:3, :], in_=xc.unsqueeze(1).to_broadcast([P, 3, TPC]))
@@ -250,7 +234,7 @@ def tile_orthogonallyattenuatedlinear_t_kernel(tc, x, weights, bias, center, sig
             if not ok(j):
                 return
             tp = ps_b.tile([P, P], BF16, name="zt", tag="b")
-            nc.tensor.transpose(tp[:], z[j % 3][:], ident_b[:])
+            nc.tensor.transpose(tp[:], z[:, j % 3, :], ident_b[:])
             st[("zt", j)] = tp
 
         def z_out(j):
@@ -324,13 +308,15 @@ def tile_orthogonallyattenuatedlinear_t_kernel(tc, x, weights, bias, center, sig
                                     op0=ALU.mult)
         wn_tp = words_transposed(wn, "wn", ps_b, "b")
         ev(0, [1])
-        nc.vector.quantize_mx(out=w_codes[:].bitcast(FP8X4), scales=w_scales[:], in_=w_grp[:])
         nc.vector.reciprocal(out=rs[:], in_=sg_ps[:, :, 0])
-        quant(0)
+        nc.vector.quantize_mx(out=w_codes[:].bitcast(FP8X4), scales=w_scales[:], in_=w_grp[:])
         nc.vector.scalar_tensor_tensor(out=coef[:, 0, :], in0=rs[:], scalar=-1.0, in1=rs[:],
                                        op0=ALU.mult, op1=ALU.mult)
         words_out(wn_tp, wn_grp, nc.vector.tensor_copy)
+        nc.vector.tensor_tensor(out=coef[:, 1, :], in0=coef[:, 0, :], in1=c2[:], op=ALU.mult)
+        quant(0)
         t1(1)
+        nc.vector.tensor_copy(out=pc[:, :, :, 0], in_=coef[:])
         cw_ps = ps_t.tile([P, 2, P], F32, name="cw_ps", tag="tb")
         c4 = c_grp[:].rearrange("p (c t) -> p c t", t=4)
         w4 = w_grp[:].rearrange("p (c t) -> p c t", t=4)
@@ -340,25 +326,24 @@ def tile_orthogonallyattenuatedlinear_t_kernel(tc, x, weights, bias, center, sig
                                  start=t == 0, stop=t == 3)
         m_a(0, 0)
         nc.vector.quantize_mx(out=wn_codes[:].bitcast(FP8X4), scales=wn_scales[:], in_=wn_grp[:])
-        for h in range(2):
-            nc.vector.scalar_tensor_tensor(out=junk_c[:], in0=cw_ps[:, h, :], scalar=rinv[:, h:h + 1], in1=ident_f[:],
-                                           op0=ALU.mult, op1=ALU.mult, accum_out=cw[:, h:h + 1])
-        nc.vector.scalar_tensor_tensor(out=is2x2[:], in0=rs[:], scalar=2.0, in1=rs[:], op0=ALU.mult, op1=ALU.mult)
-        nc.vector.scalar_tensor_tensor(out=nb[:], in0=cw[:], scalar=-1.0, in1=rs[:], op0=ALU.mult, op1=ALU.mult)
+        nc.vector.tensor_tensor(out=res[:], in0=coef[:], in1=pc[:, :, :, 0], op=ALU.subtract)
         nc.vector.quantize_mx(out=c_codes[:].bitcast(FP8X4), scales=c_scales[:], in_=c_grp[:])
+        nc.vector.tensor_copy(out=pc[:, :, :, 1], in_=res[:])
         m_bc(0, 0, "b")
         m_bc(0, 1, "b")
         m_bc(0, 0, "c")
-        nc.gpsimd.tensor_tensor(out=coef[:, 1, :], in0=coef[:, 0, :], in1=c2[:], op=ALU.mult)
-        nc.gpsimd.tensor_copy(out=pc[:, :, :, 0], in_=coef[:])
-        nc.gpsimd.tensor_tensor(out=res[:], in0=coef[:], in1=pc[:, :, :, 0], op=ALU.subtract)
-        nc.gpsimd.tensor_copy(out=pc[:, :, :, 1], in_=res[:])
-        nc.gpsimd.tensor_tensor(out=pc[:, :, :, 2], in0=res[:], in1=pc[:, :, :, 1], op=ALU.subtract)
+        for h in range(2):
+            nc.vector.scalar_tensor_tensor(out=junk_c[:], in0=cw_ps[:, h, :], scalar=rinv[:, h:h + 1], in1=ident_f[:],
+                                           op0=ALU.mult, op1=ALU.mult, accum_out=cw[:, h:h + 1])
+            if h == 0:
+                nc.vector.tensor_tensor(out=pc[:, :, :, 2], in0=res[:], in1=pc[:, :, :, 1], op=ALU.subtract)
+        nc.vector.scalar_tensor_tensor(out=is2x2[:], in0=rs[:], scalar=2.0, in1=rs[:], op0=ALU.mult, op1=ALU.mult)
         for k0, count in [(0, 3), (3, 2), (5, 1)]:
-            nc.gpsimd.tensor_copy(
+            nc.vector.tensor_copy(
                 out=zr[:, :, k0 * TPC:(k0 + count) * TPC].rearrange("p h (k t) -> p h k t", t=TPC),
                 in_=pc[:, 0, :, 0:count].unsqueeze(3).to_broadcast([P, 2, count, TPC]))
-        nc.gpsimd.tensor_copy(out=zr[:, :, NK * TPC:NK * TPC + 3], in_=pc[:, 1, :, :])
+        nc.vector.tensor_copy(out=zr[:, :, NK * TPC:NK * TPC + 3], in_=pc[:, 1, :, :])
+        nc.vector.scalar_tensor_tensor(out=nb[:], in0=cw[:], scalar=-1.0, in1=rs[:], op0=ALU.mult, op1=ALU.mult)
         z_split(0)
         x2_rows(1, [0, 1, 2])
         sq(0, 0)
@@ -367,15 +352,14 @@ def tile_orthogonallyattenuatedlinear_t_kernel(tc, x, weights, bias, center, sig
         for h in range(2):
             nc.tensor.transpose(rk_ps[:, h * P:(h + 1) * P], zr[:, h, :], ident_b[:])
         nc.scalar.copy(out=zrt[:], in_=rk_ps[:])
-        for t in range(TPC):
-            nc.gpsimd.tensor_scalar(out=rk[:, t, :], in0=zrt[:], scalar1=mask[:, t:t + 1], scalar2=0.0,
-                                    op0=ALU.mult, op1=ALU.add)
         ev(1, [0])
         ev(1, [1])
         t1(2)
         z_t(0)
         x2_rows(1, [3])
         quant(1)
+        for t in range(TPC):
+            nc.vector.tensor_scalar(out=rk[:, t, :], in0=zrt[:], scalar1=mask[:, t:t + 1], scalar2=None, op0=ALU.mult)
         z_out(0)
         m_bc(1, 0, "b")
         m_bc(1, 1, "b")
@@ -397,12 +381,10 @@ def tile_orthogonallyattenuatedlinear_t_kernel(tc, x, weights, bias, center, sig
             t1(j + 3)
             z_t(j + 1)
             t2_tr(j)
-            x2_rows(j + 2, [1, 2] if j in (1, 3,) else [1, 2, 3])
+            x2_rows(j + 2, [1, 2, 3])
             pw_op(j, 1)
             ex(j, 0, 2)
             ex(j, 2, 2)
-            if j in (1, 3):
-                x2_vec(j + 2, 3)
             m_bc(j + 1, 0, "c")
             m_a(j + 1, 0)
             quant(j + 2)

@@ -134,9 +134,19 @@ def tile_orthogonallyattenuatedlinear_t_kernel(tc, x, weights, bias, center, sig
             if not ok(j):
                 return
             for t in tiles:
+                if ("x2", j, t) in st:
+                    continue
+                st[("x2", j, t)] = True
                 junk = work.tile([P, K], BF16, name="junk", tag="junk")
                 nc.scalar.activation(out=junk[:], in_=x_sb[j][:, t * K:(t + 1) * K], func=ACT.Square,
                                      accum_out=x2[:, j * TPC + t:j * TPC + t + 1])
+
+        def x2_vec(j, t):
+            if not ok(j):
+                return
+            xt = x_sb[j][:, t * K:(t + 1) * K]
+            nc.vector.scalar_tensor_tensor(out=junk_v[:], in0=xt, scalar=1.0, in1=xt, op0=ALU.mult, op1=ALU.mult,
+                                           accum_out=x2[:, j * TPC + t:j * TPC + t + 1])
 
         def t1(j, halves=(0, 1)):
             if not ok(j):
@@ -209,7 +219,12 @@ def tile_orthogonallyattenuatedlinear_t_kernel(tc, x, weights, bias, center, sig
             u_sb = work.tile([P, CW], F32, name="u_sb", tag="u_sb", bufs=4)
             nc.vector.scalar_tensor_tensor(out=u_sb[:], in0=st[("c", j, h)][:], scalar=is2x2[:, h:h + 1],
                                            in1=st[("t2", j, h)][:], op0=ALU.mult, op1=ALU.add)
-            st[("u", j, h)] = u_sb
+            st[("u", j, h)] = [u_sb]
+
+        def u_parts(j, h):
+            u_sb = work.tile([P, CW], F32, name="u_sb", tag="u_sb", bufs=4)
+            nc.scalar.activation(out=u_sb[:], in_=st[("c", j, h)][:], func=ACT.Identity, scale=is2x2[:, h:h + 1])
+            st[("u", j, h)] = [st[("t2", j, h)], u_sb]
 
         def pw_op(j, b):
             if not ok(j):
@@ -220,6 +235,9 @@ def tile_orthogonallyattenuatedlinear_t_kernel(tc, x, weights, bias, center, sig
                                     in1=bias_b, op=ALU.add)
 
         def z_split(j):
+            if ("z", j) in st:
+                return
+            st[("z", j)] = True
             if not ok(j):
                 return
             zt = z[:, j % 3, :].rearrange("p (k t) -> p k t", t=TPC)
@@ -227,7 +245,8 @@ def tile_orthogonallyattenuatedlinear_t_kernel(tc, x, weights, bias, center, sig
             r1 = work.tile([P, TPC], F32, name="r1", tag="r1")
             nc.gpsimd.tensor_copy(out=zt[:, 0:3, :], in_=xc.unsqueeze(1).to_broadcast([P, 3, TPC]))
             nc.gpsimd.tensor_tensor(out=r1[:], in0=xc, in1=zt[:, 0, :], op=ALU.subtract)
-            nc.gpsimd.tensor_copy(out=zt[:, 3:5, :], in_=r1[:].unsqueeze(1).to_broadcast([P, 2, TPC]))
+            nc.gpsimd.tensor_tensor(out=zt[:, 3:5, :], in0=xc.unsqueeze(1).to_broadcast([P, 2, TPC]), in1=zt[:, 0:2, :],
+                                    op=ALU.subtract)
             nc.gpsimd.tensor_tensor(out=zt[:, 5, :], in0=r1[:], in1=zt[:, 3, :], op=ALU.subtract)
 
         def z_t(j):
@@ -259,15 +278,17 @@ def tile_orthogonallyattenuatedlinear_t_kernel(tc, x, weights, bias, center, sig
                 for tt in range(2):
                     for h in range(2):
                         t = 2 * b + tt
-                        nc.tensor.matmul(st[("tb", j, b)][:, tt, h * P:(h + 1) * P],
-                                         lhsT=st[("u", j, h)][:, t * P:(t + 1) * P], rhs=ident_f[:],
-                                         is_transpose=True, start=False, stop=tt == 1 and h == 1)
+                        terms = st[("u", j, h)]
+                        for part in terms:
+                            nc.tensor.matmul(st[("tb", j, b)][:, tt, h * P:(h + 1) * P],
+                                             lhsT=part[:, t * P:(t + 1) * P], rhs=ident_f[:], is_transpose=True,
+                                             start=False, stop=tt == 1 and h == 1 and part is terms[-1])
 
         def ex(j, t0, nt):
             if not ok(j):
                 return
             if t0 == 0:
-                st[("om", j)] = work.tile([P, TPC, N], F32, name="om", tag="om")
+                st[("om", j)] = work.tile([P, TPC, N], F32, name="om", tag="om", bufs=3)
             nc.scalar.activation(out=st[("om", j)][:, t0:t0 + nt, :],
                                  in_=st[("tb", j, t0 // 2)][:, t0 % 2:t0 % 2 + nt, :], func=ACT.Exp)
 
@@ -367,6 +388,8 @@ def tile_orthogonallyattenuatedlinear_t_kernel(tc, x, weights, bias, center, sig
 
         for j in range(NCH - 3):
             ev(j + 2, [0])
+            if j in (1, 3):
+                x2_vec(j + 3, 3)
             u_op(j, 0)
             t2_mm(j, 0)
             m_bc(j, 1, "c")
@@ -381,7 +404,7 @@ def tile_orthogonallyattenuatedlinear_t_kernel(tc, x, weights, bias, center, sig
             t1(j + 3)
             z_t(j + 1)
             t2_tr(j)
-            x2_rows(j + 2, [1, 2, 3])
+            x2_rows(j + 2, [1, 2] if j in (2, 4) else [1, 2, 3])
             pw_op(j, 1)
             ex(j, 0, 2)
             ex(j, 2, 2)
@@ -434,13 +457,13 @@ def tile_orthogonallyattenuatedlinear_t_kernel(tc, x, weights, bias, center, sig
         pw_op(i, 1)
         t2_mm(i, 1)
         m_bc(j, 1, "c", spare)
-        z_t(j)
         t2_tr(i)
+        z_t(j)
+        u_parts(j, 0)
         ex(i, 0, 2)
         ex(i, 2, 2)
-        u_op(j, 0)
-        z_out(j)
         u_op(j, 1)
+        z_out(j)
         m_a(j, 0)
         m_a(j, 1, spare)
         t2_mm(j, 0, (ps_b, "b"))
@@ -448,7 +471,7 @@ def tile_orthogonallyattenuatedlinear_t_kernel(tc, x, weights, bias, center, sig
         t2_tr(j)
         pw_op(j, 0)
         pw_op(j, 1)
-        mul(i, 0, 2, nc.gpsimd)
+        mul(i, 0, 2, nc.vector)
         mul(i, 2, 2, nc.vector)
         for t in range(TPC):
             ex(j, t, 1)

@@ -230,7 +230,7 @@ def tile_orthogonallyattenuatedlinear_t_kernel(tc, x, weights, bias, center, sig
             if not ok(j):
                 return
             if b == 0:
-                st[("pw", j)] = work.tile([P, TPC, N], F32, name="pw", tag="pw", bufs=3)
+                st[("pw", j)] = work.tile([P, TPC, N], F32, name="pw", tag="pw", bufs=4)
             nc.vector.tensor_tensor(out=st[("pw", j)][:, 2 * b:2 * b + 2, :], in0=st[("a", j, b)][:],
                                     in1=bias_b, op=ALU.add)
 
@@ -288,7 +288,7 @@ def tile_orthogonallyattenuatedlinear_t_kernel(tc, x, weights, bias, center, sig
             if not ok(j):
                 return
             if t0 == 0:
-                st[("om", j)] = work.tile([P, TPC, N], F32, name="om", tag="om", bufs=3)
+                st[("om", j)] = work.tile([P, TPC, N], F32, name="om", tag="om", bufs=4)
             nc.scalar.activation(out=st[("om", j)][:, t0:t0 + nt, :],
                                  in_=st[("tb", j, t0 // 2)][:, t0 % 2:t0 % 2 + nt, :], func=ACT.Exp)
 
@@ -296,7 +296,7 @@ def tile_orthogonallyattenuatedlinear_t_kernel(tc, x, weights, bias, center, sig
             if not ok(j):
                 return
             if t0 == 0:
-                st[("o", j)] = work.tile([P, TPC, N], F32, name="o_sb", tag="o_sb", bufs=3)
+                st[("o", j)] = work.tile([P, TPC, N], F32, name="o_sb", tag="o_sb", bufs=4)
             sl = slice(t0, t0 + nt)
             eng.tensor_tensor(out=st[("o", j)][:, sl, :], in0=st[("pw", j)][:, sl, :],
                               in1=st[("om", j)][:, sl, :], op=ALU.mult)
@@ -311,6 +311,9 @@ def tile_orthogonallyattenuatedlinear_t_kernel(tc, x, weights, bias, center, sig
                                        op0=ALU.mult, op1=ALU.mult, accum_out=ss[:, 1:2])
         nc.gpsimd.tensor_scalar_max(out=ss[:], in0=ss[:], scalar1=1e-24)
         nc.gpsimd.tensor_tensor(out=rinv[:], in0=ss[:], in1=mhalf[:], op=ALU.pow)
+        warm = ps_c.tile([P, P], F32, name="warm", tag="c")
+        for i in range(3):
+            nc.tensor.matmul(warm[:], lhsT=ident_f[:], rhs=ident_f[:], start=True, stop=True)
         w_tp = words_transposed(w_sb, "w")
         words_out(w_tp, w_grp, nc.vector.tensor_copy)
         t1(0)
@@ -388,7 +391,7 @@ def tile_orthogonallyattenuatedlinear_t_kernel(tc, x, weights, bias, center, sig
 
         for j in range(NCH - 3):
             ev(j + 2, [0])
-            if j in (1, 3):
+            if j == 1:
                 x2_vec(j + 3, 3)
             u_op(j, 0)
             t2_mm(j, 0)
@@ -404,18 +407,19 @@ def tile_orthogonallyattenuatedlinear_t_kernel(tc, x, weights, bias, center, sig
             t1(j + 3)
             z_t(j + 1)
             t2_tr(j)
-            x2_rows(j + 2, [1, 2] if j in (2, 4) else [1, 2, 3])
+            x2_rows(j + 2, [1, 2] if j == 2 else [1, 2, 3])
             pw_op(j, 1)
             ex(j, 0, 2)
             ex(j, 2, 2)
             m_bc(j + 1, 0, "c")
             m_a(j + 1, 0)
             quant(j + 2)
+            mul(j - 1, 3, 1, nc.vector)
             z_out(j + 1)
             m_bc(j + 2, 0, "b")
             m_bc(j + 2, 1, "b")
             z_split(j + 2)
-            mul(j, 0, TPC, nc.gpsimd)
+            mul(j, 0, 3, nc.gpsimd)
 
         g, i, j = NCH - 3, NCH - 2, NCH - 1
         spare = (ps_x, "xt")
@@ -439,6 +443,7 @@ def tile_orthogonallyattenuatedlinear_t_kernel(tc, x, weights, bias, center, sig
         ex(g, 0, 2)
         ex(g, 2, 2)
         quant(j)
+        mul(g - 1, 3, 1, nc.vector)
         z_out(i)
         m_bc(i, 0, "c")
         m_a(i, 0)

from contextlib import ExitStack

import concourse.masks as masks
import concourse.mybir as mybir

FP8X4 = mybir.dt.float8_e4m3fn_x4
BF16 = mybir.dt.bfloat16
F32 = mybir.dt.float32
U32 = mybir.dt.uint32
U8 = mybir.dt.uint8
ALU = mybir.AluOpType
ACT = mybir.ActivationFunctionType

P = 128
M, K, N = 4096, 512, 256
FLOPS = 3 * 2 * M * K * N
TPC = 4
NCH = M // (P * TPC)
CW = P * TPC
NK = 6


def tile_orthogonallyattenuatedlinear_t_kernel(tc, x, weights, bias, center, sigma, out):
    nc = tc.nc
    with ExitStack() as ctx:
        const = ctx.enter_context(tc.tile_pool(name="const", bufs=1))
        xpool = ctx.enter_context(tc.tile_pool(name="xpool", bufs=1))
        work = ctx.enter_context(tc.tile_pool(name="work", bufs=2))
        ps_x = ctx.enter_context(tc.psum_pool(name="ps_x", bufs=2))
        ps_b = ctx.enter_context(tc.psum_pool(name="ps_b", bufs=2))
        ps_c = ctx.enter_context(tc.psum_pool(name="ps_c", bufs=1))
        ps_a = ctx.enter_context(tc.psum_pool(name="ps_a", bufs=1))
        ps_t = ctx.enter_context(tc.psum_pool(name="ps_t", bufs=2))
        ctx.enter_context(tc.manual_schedule())

        xv = x.rearrange("(p c t) k -> p c (t k)", c=NCH, t=TPC)
        ov = out.rearrange("(p c t) n -> p c (t n)", c=NCH, t=TPC)

        w_sb = const.tile([P, 2 * K], BF16, name="w_sb")
        c_sb = const.tile([P, 2 * K], BF16, name="c_sb")
        sig = const.tile([P, N], BF16, name="sig")
        bias_sb = const.tile([P, N], BF16, name="bias_sb")
        one1 = const.tile([P, 1], F32, name="one1")
        nc.vector.memset(one1[:], 1.0)
        nc.vector.memset(sig[:], 0.0)
        x_sb = [xpool.tile([P, TPC * K], BF16, name="x%d" % c) for c in range(NCH)]

        def load_x(c, pieces):
            width = TPC * K // pieces
            for s in range(pieces):
                nc.sync.dma_start(out=x_sb[c][:, s * width:(s + 1) * width], in_=xv[:, c, s * width:(s + 1) * width])

        for h in range(2):
            nc.sync.dma_start(out=w_sb[:, h * K:(h + 1) * K], in_=weights[h * P:(h + 1) * P, :])
        load_x(0, 2)
        nc.sync.dma_start(out=sig[0:1, :], in_=sigma.unsqueeze(0))
        nc.sync.dma_start(out=c_sb[:].rearrange("p (h k) -> p h k", h=2),
                          in_=center.rearrange("(h p) k -> p h k", h=2))
        for c in range(1, NCH):
            if c == 4:
                nc.sync.dma_start(out=bias_sb[:], in_=bias.partition_broadcast(P))
            load_x(c, 1)

        dummy = const.tile([P, 1], F32, name="dummy")
        nc.scalar.activation(out=dummy[:], in_=one1[:], func=ACT.Exp)
        mhalf = const.tile([P, 2], F32, name="mhalf")
        nc.vector.memset(mhalf[:], -0.5)
        ident_f = const.tile([P, P], F32, name="ident_f")
        masks.make_identity(nc, ident_f[:])
        ident_b = const.tile([P, P], BF16, name="ident_b")
        nc.vector.tensor_copy(out=ident_b[:], in_=ident_f[:])
        x2 = const.tile([P, NCH * TPC], F32, name="x2")

        def quantised(name, width):
            codes = const.tile([P, 32 + width], U32, name=name + "_codes", align_bytes=256)
            scales = const.tile([P, 192 + width], U8, name=name + "_scales", align_bytes=256)
            return codes[:, 32:32 + width], scales[:, 192:192 + width]

        junk_w = const.tile([P, K], BF16, name="junk_w")
        junk_c = const.tile([P, P], F32, name="junk_c")
        junk_v = const.tile([P, K], BF16, name="junk_v")
        ss = const.tile([P, 2], F32, name="ss")
        c2 = const.tile([P, 2], F32, name="c2")
        cw = const.tile([P, 2], F32, name="cw")
        rinv = const.tile([P, 2], F32, name="rinv")
        nb = const.tile([P, 2], F32, name="nb")
        w_codes, w_scales = quantised("w", N)
        c_codes, c_scales = quantised("c", N)
        wn_codes, wn_scales = quantised("wn", N)
        w_grp = const.tile([P, 4 * N], BF16, name="w_grp", align_bytes=64)
        c_grp = const.tile([P, 4 * N], BF16, name="c_grp", align_bytes=64)
        wn_grp = const.tile([P, 4 * N], BF16, name="wn_grp", align_bytes=64)
        wn = const.tile([P, 2 * K], BF16, name="wn")
        rs = const.tile([P, 2], F32, name="rs")
        is2x2 = const.tile([P, 2], F32, name="is2x2")
        coef = const.tile([P, 2, 2], F32, name="coef")
        res = const.tile([P, 2, 2], F32, name="res")
        pc = const.tile([P, 2, 2, 3], BF16, name="pc")
        zr = const.tile([P, 2, P], BF16, name="zr")
        zrt = const.tile([P, N], BF16, name="zrt")
        mask = const.tile([P, TPC], F32, name="mask")
        mask_c = const.tile([P, 1], F32, name="mask_c")
        nc.vector.tensor_reduce(out=mask[:], in_=ident_f[:, 0:NK * TPC].rearrange("p (k t) -> p t k", t=TPC),
                                op=ALU.add, axis=mybir.AxisListType.X)
        nc.vector.tensor_reduce(out=mask_c[:], in_=ident_f[:, NK * TPC:NK * TPC + 3],
                                op=ALU.add, axis=mybir.AxisListType.X)
        nc.vector.tensor_scalar(out=mask[:], in0=mask[:], scalar1=mask_c[:], scalar2=None, op0=ALU.add)
        rk = const.tile([P, TPC, N], BF16, name="rk")
        nc.vector.memset(zr[:], 0.0)
        z = const.tile([P, 3, P], BF16, name="z")
        nc.vector.memset(z[:], 0.0)
        nc.vector.memset(z[:, :, NK * TPC:NK * TPC + 3], 1.0)
        bias_b = bias_sb[:].unsqueeze(1).to_broadcast([P, 2, N])

        def words_transposed(src, name, pool=ps_t, tag="tb"):
            src_f = src[:].bitcast(F32)
            tp = pool.tile([P, 2, N], F32, name=name + "_tp", tag=tag)
            for h in range(2):
                for u in range(2):
                    nc.tensor.transpose(tp[:, u, h * P:(h + 1) * P],
                                        src_f[:, h * 256 + u * P:h * 256 + (u + 1) * P], ident_f[:])
            return tp

        def words_out(tp, grp, copy):
            copy(out=grp[:].bitcast(F32).rearrange("p (c u) -> p c u", u=2),
                                  in_=tp[:].rearrange("p u c -> p c u"))

        st = {}

        def ok(j):
            return 0 <= j < NCH

        def x2_rows(j, tiles):
            if not ok(j):
                return
            for t in tiles:
                if ("x2", j, t) in st:
                    continue
                st[("x2", j, t)] = True
                junk = work.tile([P, K], BF16, name="junk", tag="junk")
                nc.scalar.activation(out=junk[:], in_=x_sb[j][:, t * K:(t + 1) * K], func=ACT.Square,
                                     accum_out=x2[:, j * TPC + t:j * TPC + t + 1])

        def x2_vec(j, t):
            if not ok(j):
                return
            xt = x_sb[j][:, t * K:(t + 1) * K]
            nc.vector.scalar_tensor_tensor(out=junk_v[:], in0=xt, scalar=1.0, in1=xt, op0=ALU.mult, op1=ALU.mult,
                                           accum_out=x2[:, j * TPC + t:j * TPC + t + 1])

        def t1(j, halves=(0, 1)):
            if not ok(j):
                return
            x_f = x_sb[j][:].bitcast(F32)
            for b in halves:
                tp = ps_x.tile([P, 2, 2 * P], F32, name="xt", tag="xt")
                for tt in range(2):
                    for u in range(2):
                        col = (2 * b + tt) * 256 + u * P
                        nc.tensor.transpose(tp[:, u, tt * P:(tt + 1) * P], x_f[:, col:col + P], ident_f[:])
                st[("xt", j, b)] = tp

        def ev(j, halves=(0, 1)):
            if not ok(j):
                return
            for b in halves:
                if b == 0:
                    st[("grp", j)] = work.tile([P, 4 * CW], BF16, name="grp", tag="grp", bufs=3, align_bytes=64)
                g3 = st[("grp", j)][:].bitcast(F32).rearrange("p (c u) -> p c u", u=2)
                nc.vector.tensor_copy(out=g3[:, b * 2 * P:(b + 1) * 2 * P, :],
                                      in_=st[("xt", j, b)][:].rearrange("p u c -> p c u"))

        def quant(j):
            if not ok(j):
                return
            codes = work.tile([P, CW], U32, name="xcodes", tag="xcodes", bufs=4, align_bytes=256)
            scales_tile = work.tile([P, 64 + CW], U8, name="xscales", tag="xscales", bufs=4, align_bytes=256)
            scales = scales_tile[:, 64:64 + CW]
            nc.vector.quantize_mx(out=codes[:].bitcast(FP8X4), scales=scales[:], in_=st[("grp", j)][:])
            st[("q", j)] = (codes, scales)

        def m_a(j, b, bank=None):
            if not ok(j) or ("a", j, b) in st:
                return
            codes, scales = st[("q", j)]
            pool, tag = bank or (ps_a, "a")
            acc = pool.tile([P, 2, N], F32, name="a", tag=tag)
            for tt in range(2):
                cols = slice((2 * b + tt) * P, (2 * b + tt + 1) * P)
                nc.tensor.matmul_mx(out=acc[:, tt, :], lhsT=codes[:, cols].bitcast(FP8X4),
                                    lhsT_scale=scales[:, cols],
                                    rhs=w_codes[:].bitcast(FP8X4), rhs_scale=w_scales[:],
                                    start=True, stop=True)
            st[("a", j, b)] = acc

        def m_bc(j, h, nm, bank=None):
            if not ok(j) or (nm, j, h) in st:
                return
            codes, scales = st[("q", j)]
            cd, sc = (wn_codes, wn_scales) if nm == "b" else (c_codes, c_scales)
            cols = slice(h * P, (h + 1) * P)
            pool, tag = bank or ((ps_b, "b") if nm == "b" else (ps_c, "c"))
            acc = pool.tile([P, CW], F32, name=nm, tag=tag)
            nc.tensor.matmul_mx(out=acc[:], lhsT=cd[:, cols].bitcast(FP8X4), lhsT_scale=sc[:, cols],
                                rhs=codes[:].bitcast(FP8X4), rhs_scale=scales[:], start=True, stop=True)
            st[(nm, j, h)] = acc

        def sq(j, h):
            if not ok(j):
                return
            t2 = work.tile([P, CW], F32, name="t2", tag="t2", bufs=4)
            nc.scalar.activation(out=t2[:], in_=st[("b", j, h)][:], func=ACT.Square,
                                 bias=nb[:, h:h + 1], scale=rs[:, h:h + 1])
            st[("t2", j, h)] = t2

        def u_op(j, h):
            if not ok(j):
                return
            u_sb = work.tile([P, CW], F32, name="u_sb", tag="u_sb", bufs=4)
            nc.vector.scalar_tensor_tensor(out=u_sb[:], in0=st[("c", j, h)][:], scalar=is2x2[:, h:h + 1],
                                           in1=st[("t2", j, h)][:], op0=ALU.mult, op1=ALU.add)
            st[("u", j, h)] = [u_sb]

        def u_parts(j, h):
            u_sb = work.tile([P, CW], F32, name="u_sb", tag="u_sb", bufs=4)
            nc.scalar.activation(out=u_sb[:], in_=st[("c", j, h)][:], func=ACT.Identity, scale=is2x2[:, h:h + 1])
            st[("u", j, h)] = [st[("t2", j, h)], u_sb]

        def pw_op(j, b):
            if not ok(j):
                return
            if b == 0:
                st[("pw", j)] = work.tile([P, TPC, N], F32, name="pw", tag="pw", bufs=4)
            nc.vector.tensor_tensor(out=st[("pw", j)][:, 2 * b:2 * b + 2, :], in0=st[("a", j, b)][:],
                                    in1=bias_b, op=ALU.add)

        def z_split(j):
            if ("z", j) in st:
                return
            st[("z", j)] = True
            if not ok(j):
                return
            zt = z[:, j % 3, :].rearrange("p (k t) -> p k t", t=TPC)
            xc = x2[:, j * TPC:(j + 1) * TPC]
            r1 = work.tile([P, TPC], F32, name="r1", tag="r1")
            nc.gpsimd.tensor_copy(out=zt[:, 0:3, :], in_=xc.unsqueeze(1).to_broadcast([P, 3, TPC]))
            nc.gpsimd.tensor_tensor(out=r1[:], in0=xc, in1=zt[:, 0, :], op=ALU.subtract)
            nc.gpsimd.tensor_tensor(out=zt[:, 3:5, :], in0=xc.unsqueeze(1).to_broadcast([P, 2, TPC]), in1=zt[:, 0:2, :],
                                    op=ALU.subtract)
            nc.gpsimd.tensor_tensor(out=zt[:, 5, :], in0=r1[:], in1=zt[:, 3, :], op=ALU.subtract)

        def z_t(j):
            if not ok(j):
                return
            tp = ps_b.tile([P, P], BF16, name="zt", tag="b")
            nc.tensor.transpose(tp[:], z[:, j % 3, :], ident_b[:])
            st[("zt", j)] = tp

        def z_out(j):
            if not ok(j):
                return
            zs = work.tile([P, P], BF16, name="zs", tag="zs", bufs=3)
            nc.vector.tensor_copy(out=zs[:], in_=st[("zt", j)][:])
            st[("zs", j)] = zs

        def t2_mm(j, b, bank=None):
            if not ok(j):
                return
            pool, tag = bank or (ps_t, "tb")
            tp = pool.tile([P, 2, N], F32, name="tb", tag=tag)
            nc.tensor.matmul(tp[:], lhsT=st[("zs", j)][:], rhs=rk[:, 2 * b:2 * b + 2, :], start=True, stop=False)
            st[("tb", j, b)] = tp

        def t2_tr(j):
            if not ok(j):
                return
            for b in range(2):
                for tt in range(2):
                    for h in range(2):
                        t = 2 * b + tt
                        terms = st[("u", j, h)]
                        for part in terms:
                            nc.tensor.matmul(st[("tb", j, b)][:, tt, h * P:(h + 1) * P],
                                             lhsT=part[:, t * P:(t + 1) * P], rhs=ident_f[:], is_transpose=True,
                                             start=False, stop=tt == 1 and h == 1 and part is terms[-1])

        def ex(j, t0, nt):
            if not ok(j):
                return
            if t0 == 0:
                st[("om", j)] = work.tile([P, TPC, N], F32, name="om", tag="om", bufs=4)
            nc.scalar.activation(out=st[("om", j)][:, t0:t0 + nt, :],
                                 in_=st[("tb", j, t0 // 2)][:, t0 % 2:t0 % 2 + nt, :], func=ACT.Exp)

        def mul(j, t0, nt, eng):
            if not ok(j):
                return
            if t0 == 0:
                st[("o", j)] = work.tile([P, TPC, N], F32, name="o_sb", tag="o_sb", bufs=4)
            sl = slice(t0, t0 + nt)
            eng.tensor_tensor(out=st[("o", j)][:, sl, :], in0=st[("pw", j)][:, sl, :],
                              in1=st[("om", j)][:, sl, :], op=ALU.mult)
            nc.sync.dma_start(out=ov[:, j, t0 * N:(t0 + nt) * N],
                              in_=st[("o", j)][:, sl, :].rearrange("p t n -> p (t n)"))

        def w_half(t, h):
            return t[:, h * K:(h + 1) * K]

        nc.scalar.activation(out=junk_w[:], in_=w_half(w_sb, 0), func=ACT.Square, accum_out=ss[:, 0:1])
        nc.vector.scalar_tensor_tensor(out=junk_v[:], in0=w_half(w_sb, 1), scalar=1.0, in1=w_half(w_sb, 1),
                                       op0=ALU.mult, op1=ALU.mult, accum_out=ss[:, 1:2])
        nc.gpsimd.tensor_scalar_max(out=ss[:], in0=ss[:], scalar1=1e-24)
        nc.gpsimd.tensor_tensor(out=rinv[:], in0=ss[:], in1=mhalf[:], op=ALU.pow)
        warm = ps_c.tile([P, P], F32, name="warm", tag="c")
        for i in range(3):
            nc.tensor.matmul(warm[:], lhsT=ident_f[:], rhs=ident_f[:], start=True, stop=True)
        w_tp = words_transposed(w_sb, "w")
        words_out(w_tp, w_grp, nc.vector.tensor_copy)
        t1(0)
        sg_ps = ps_a.tile([P, 2, P], BF16, name="sg_ps", tag="a")
        for h in range(2):
            nc.tensor.transpose(sg_ps[:, h, :], sig[:, h * P:(h + 1) * P], ident_b[:])
        c_tp = words_transposed(c_sb, "c")
        x2_rows(0, [0, 1])
        nc.scalar.activation(out=junk_w[:], in_=w_half(c_sb, 0), func=ACT.Square, accum_out=c2[:, 0:1])
        nc.scalar.activation(out=junk_w[:], in_=w_half(c_sb, 1), func=ACT.Square, accum_out=c2[:, 1:2])
        words_out(c_tp, c_grp, nc.scalar.copy)
        x2_rows(0, [2, 3])
        ev(0, [0])
        for h in range(2):
            nc.vector.tensor_scalar(out=w_half(wn, h), in0=w_half(w_sb, h), scalar1=rinv[:, h:h + 1], scalar2=None,
                                    op0=ALU.mult)
        wn_tp = words_transposed(wn, "wn", ps_b, "b")
        ev(0, [1])
        nc.vector.reciprocal(out=rs[:], in_=sg_ps[:, :, 0])
        nc.vector.quantize_mx(out=w_codes[:].bitcast(FP8X4), scales=w_scales[:], in_=w_grp[:])
        nc.vector.scalar_tensor_tensor(out=coef[:, 0, :], in0=rs[:], scalar=-1.0, in1=rs[:],
                                       op0=ALU.mult, op1=ALU.mult)
        words_out(wn_tp, wn_grp, nc.vector.tensor_copy)
        nc.vector.tensor_tensor(out=coef[:, 1, :], in0=coef[:, 0, :], in1=c2[:], op=ALU.mult)
        quant(0)
        t1(1)
        nc.vector.tensor_copy(out=pc[:, :, :, 0], in_=coef[:])
        cw_ps = ps_t.tile([P, 2, P], F32, name="cw_ps", tag="tb")
        c4 = c_grp[:].rearrange("p (c t) -> p c t", t=4)
        w4 = w_grp[:].rearrange("p (c t) -> p c t", t=4)
        for h in range(2):
            for t in range(4):
                nc.tensor.matmul(cw_ps[:, h, :], lhsT=c4[:, h * P:(h + 1) * P, t], rhs=w4[:, h * P:(h + 1) * P, t],
                                 start=t == 0, stop=t == 3)
        m_a(0, 0)
        nc.vector.quantize_mx(out=wn_codes[:].bitcast(FP8X4), scales=wn_scales[:], in_=wn_grp[:])
        nc.vector.tensor_tensor(out=res[:], in0=coef[:], in1=pc[:, :, :, 0], op=ALU.subtract)
        nc.vector.quantize_mx(out=c_codes[:].bitcast(FP8X4), scales=c_scales[:], in_=c_grp[:])
        nc.vector.tensor_copy(out=pc[:, :, :, 1], in_=res[:])
        m_bc(0, 0, "b")
        m_bc(0, 1, "b")
        m_bc(0, 0, "c")
        for h in range(2):
            nc.vector.scalar_tensor_tensor(out=junk_c[:], in0=cw_ps[:, h, :], scalar=rinv[:, h:h + 1], in1=ident_f[:],
                                           op0=ALU.mult, op1=ALU.mult, accum_out=cw[:, h:h + 1])
            if h == 0:
                nc.vector.tensor_tensor(out=pc[:, :, :, 2], in0=res[:], in1=pc[:, :, :, 1], op=ALU.subtract)
        nc.vector.scalar_tensor_tensor(out=is2x2[:], in0=rs[:], scalar=2.0, in1=rs[:], op0=ALU.mult, op1=ALU.mult)
        for k0, count in [(0, 3), (3, 2), (5, 1)]:
            nc.vector.tensor_copy(
                out=zr[:, :, k0 * TPC:(k0 + count) * TPC].rearrange("p h (k t) -> p h k t", t=TPC),
                in_=pc[:, 0, :, 0:count].unsqueeze(3).to_broadcast([P, 2, count, TPC]))
        nc.vector.tensor_copy(out=zr[:, :, NK * TPC:NK * TPC + 3], in_=pc[:, 1, :, :])
        nc.vector.scalar_tensor_tensor(out=nb[:], in0=cw[:], scalar=-1.0, in1=rs[:], op0=ALU.mult, op1=ALU.mult)
        z_split(0)
        x2_rows(1, [0, 1, 2])
        sq(0, 0)
        sq(0, 1)
        rk_ps = ps_t.tile([P, N], BF16, name="rk_ps", tag="tb")
        for h in range(2):
            nc.tensor.transpose(rk_ps[:, h * P:(h + 1) * P], zr[:, h, :], ident_b[:])
        nc.scalar.copy(out=zrt[:], in_=rk_ps[:])
        ev(1, [0])
        ev(1, [1])
        t1(2)
        z_t(0)
        x2_rows(1, [3])
        quant(1)
        for t in range(TPC):
            nc.vector.tensor_scalar(out=rk[:, t, :], in0=zrt[:], scalar1=mask[:, t:t + 1], scalar2=None, op0=ALU.mult)
        z_out(0)
        m_bc(1, 0, "b")
        m_bc(1, 1, "b")
        z_split(1)

        for j in range(NCH - 3):
            ev(j + 2, [0])
            if j == 1:
                x2_vec(j + 3, 3)
            u_op(j, 0)
            t2_mm(j, 0)
            m_bc(j, 1, "c")
            x2_rows(j + 2, [0])
            sq(j + 1, 0)
            sq(j + 1, 1)
            pw_op(j, 0)
            t2_mm(j, 1)
            m_a(j, 1)
            ev(j + 2, [1])
            u_op(j, 1)
            t1(j + 3)
            z_t(j + 1)
            t2_tr(j)
            x2_rows(j + 2, [1, 2] if j == 2 else [1, 2, 3])
            pw_op(j, 1)
            ex(j, 0, 2)
            ex(j, 2, 2)
            m_bc(j + 1, 0, "c")
            m_a(j + 1, 0)
            quant(j + 2)
            mul(j - 1, 3, 1, nc.vector)
            z_out(j + 1)
            m_bc(j + 2, 0, "b")
            m_bc(j + 2, 1, "b")
            z_split(j + 2)
            mul(j, 0, 3, nc.gpsimd)

        g, i, j = NCH - 3, NCH - 2, NCH - 1
        spare = (ps_x, "xt")
        ev(j, [0])
        u_op(g, 0)
        t2_mm(g, 0)
        m_bc(g, 1, "c")
        x2_rows(j, [0])
        sq(i, 0)
        sq(i, 1)
        pw_op(g, 0)
        t2_mm(g, 1)
        m_a(g, 1)
        ev(j, [1])
        u_op(g, 1)
        m_bc(i, 1, "c", spare)
        z_t(i)
        t2_tr(g)
        x2_rows(j, [1, 2, 3])
        pw_op(g, 1)
        ex(g, 0, 2)
        ex(g, 2, 2)
        quant(j)
        mul(g - 1, 3, 1, nc.vector)
        z_out(i)
        m_bc(i, 0, "c")
        m_a(i, 0)
        m_a(i, 1, spare)
        m_bc(j, 0, "b")
        m_bc(j, 1, "b")
        z_split(j)
        mul(g, 0, TPC, nc.gpsimd)
        sq(j, 0)
        sq(j, 1)
        u_op(i, 0)
        u_op(i, 1)
        t2_mm(i, 0)
        m_bc(j, 0, "c")
        pw_op(i, 0)
        pw_op(i, 1)
        t2_mm(i, 1)
        m_bc(j, 1, "c", spare)
        t2_tr(i)
        z_t(j)
        u_parts(j, 0)
        ex(i, 0, 2)
        ex(i, 2, 2)
        u_op(j, 1)
        z_out(j)
        m_a(j, 0)
        m_a(j, 1, spare)
        t2_mm(j, 0, (ps_b, "b"))
        t2_mm(j, 1, (ps_b, "b"))
        t2_tr(j)
        pw_op(j, 0)
        pw_op(j, 1)
        mul(i, 0, 2, nc.vector)
        mul(i, 2, 2, nc.vector)
        for t in range(TPC):
            ex(j, t, 1)
            mul(j, t, 1, nc.vector)
